import numpy as np
import ml_dtypes


def mxq(x, axis, fmt="e4m3"):
    dtype, down = {"e4m3": (ml_dtypes.float8_e4m3fn, 7), "e5m2": (ml_dtypes.float8_e5m2, 14)}[fmt]
    v = np.moveaxis(np.asarray(x, np.float32).astype(ml_dtypes.bfloat16).astype(np.float64), axis, -1)
    blocks = v.reshape(v.shape[:-1] + (-1, 32))
    amax = np.abs(blocks).max(-1, keepdims=True)
    byte = np.maximum(np.where(amax > 0, np.frexp(amax)[1] - 1 + 127, 0) - down, 1)
    scale = np.exp2(byte - 127.0)
    codes = (blocks / scale).astype(np.float32).astype(dtype).astype(np.float64)
    return np.moveaxis((codes * scale).reshape(v.shape), -1, axis)


WIDE = False


def mx_kscale(k):
    if not WIDE:
        return np.ones(k)
    levels = np.array([10, -10, 5, -5, 0])
    a = np.random.permutation(np.resize(levels, k // 512 * 4)).reshape(k // 512, 4)
    idx = np.arange(k)
    return np.exp2(a[idx // 512, idx % 128 // 32])


BF16 = ml_dtypes.bfloat16


def bf(x):
    return np.asarray(x, np.float32).astype(BF16)


def f64(x):
    return np.asarray(x).astype(np.float64)


B, IN_CH, OUT_CH, KH, KW, H, W_IN = 4, 16, 256, 4, 4, 35, 35
HO, WO = H - KH + 1, W_IN - KW + 1
L = HO * WO
KD = KH * KW
F = IN_CH * KD * KD
MXB = 32


def setup_inputs():
    s = mx_kscale(F)[(np.arange(IN_CH) * KD * KD) // MXB * MXB]
    u = np.exp2(np.round(np.log2(s) / 2))
    return {"x": bf(np.random.standard_normal((B, IN_CH, H, W_IN)) * u[None, :, None, None]),
            "W": bf(np.random.standard_normal((OUT_CH, F)) / np.sqrt(F) / np.repeat(u * u, KD * KD)[None, :])}


def _unfold(x):
    patches = np.stack([x[:, :, i:i + HO, j:j + WO] for i in range(KH) for j in range(KW)], axis=2)
    return patches.reshape(B, IN_CH, KD, L).transpose(0, 3, 1, 2)


def reference(x, W):
    p = _unfold(f64(x))
    outer = np.einsum("blci,blcj->blcij", p, p)
    feat = outer.reshape(B, L, F)
    out = mxq(f64(W), 1, "e4m3") @ mxq(feat, 2, "e4m3").transpose(0, 2, 1)
    return out.reshape(B, OUT_CH, HO, WO)

@@ -1,0 +1,264 @@
+from contextlib import ExitStack
+
+import concourse.mybir as mybir
+from concourse.masks import make_identity
+
+FLOPS = 2 * 256 * 4096 * 4096
+
+BF16 = mybir.dt.bfloat16
+F32 = mybir.dt.float32
+U32 = mybir.dt.uint32
+U8 = mybir.dt.uint8
+FP8X4 = mybir.dt.float8_e4m3fn_x4
+
+P = 128
+NIMG = 4
+SIDE = 35
+PIX = SIDE * SIDE
+XPITCH = 1168
+SETS = (((0, 0), (2, 2)), ((0, 1), (2, 0)), ((0, 3), (2, 3)))
+ROWS = (33, 33, 32)
+PASSES = (
+    (0, 0, False),
+    (0, 1, False),
+    (1, 0, False),
+    (1, 0, True),
+    (1, 1, False),
+    (1, 1, True),
+    (2, 0, False),
+    (2, 0, True),
+)
+
+
+def tile_fast2order_de_conv_kernel(tc, x, W, out):
+    nc = tc.nc
+    with ExitStack() as ctx:
+        const = ctx.enter_context(tc.tile_pool(name="const", bufs=1))
+        ddpool = ctx.enter_context(tc.tile_pool(name="ddpool", bufs=2))
+        mpool = ctx.enter_context(tc.tile_pool(name="mpool", bufs=3))
+        ring = ctx.enter_context(tc.tile_pool(name="ring", bufs=16))
+        wtmp = ctx.enter_context(tc.tile_pool(name="wtmp", bufs=4))
+        outpool = ctx.enter_context(tc.tile_pool(name="outpool", bufs=4))
+        banks = ctx.enter_context(tc.psum_pool(name="banks", bufs=8))
+        ctx.enter_context(tc.manual_schedule())
+
+        ident = const.tile([P, P], BF16, name="ident")
+        make_identity(nc, ident[:])
+
+        x_cn = x.rearrange("n c h w -> c n (h w)")
+        GROUPS = ((0, 1), (1, NIMG))
+        xa = [const.tile([P, n1 - n0, XPITCH], BF16, name="xa_%d" % n0) for (n0, n1) in GROUPS]
+        xbs = [
+            [const.tile([P, n1 - n0, XPITCH], BF16, name="xb%d_%d" % (k, n0)) for (n0, n1) in GROUPS]
+            for k in range(3)
+        ]
+
+        def load_shifted(tiles, g, length, shift):
+            n0, n1 = GROUPS[g]
+            for a in range(4):
+                for v in range(2):
+                    off = shift(a, v)
+                    nc.sync.dma_start(
+                        out=tiles[g][2 * a + v : P : 8, :, 0:length],
+                        in_=x_cn[:, n0:n1, off : off + length],
+                    )
+
+        def load_xa(g):
+            load_shifted(xa, g, 1152, lambda a, v: 2 * SIDE * v + a)
+
+        def load_xb(k, g):
+            load_shifted(xbs[k], g, ROWS[k] * SIDE, lambda a, v: SIDE * SETS[k][v][1])
+
+        def image_view(tiles, n):
+            return tiles[0][:, 0, :] if n == 0 else tiles[1][:, n - 1, :]
+
+        load_xa(0)
+        load_xb(0, 0)
+        load_xb(1, 0)
+        w_sb = const.tile([P, 2, 4096], BF16, name="w_sb")
+        w_view = W.rearrange("(h o) f -> o h f", h=2)
+        for h in range(2):
+            nc.sync.dma_start(out=w_sb[:, h, :], in_=w_view[:, h, :])
+        load_xb(2, 0)
+        load_xa(1)
+        for k in range(3):
+            load_xb(k, 1)
+
+        wc = const.tile([P, 2048], U32, name="wc", align_bytes=64)
+        ws = const.tile([P, 2048], U8, name="ws", align_bytes=64)
+
+        def make_dd(n):
+            dd = ddpool.tile([P, 33, 32, 2], BF16, name="dd")
+            src = image_view(xa, n)[:, 0 : 33 * SIDE].rearrange("p (r z) -> p r z", z=SIDE)[:, :, 0:32]
+            src = src.unsqueeze(3).to_broadcast([P, 33, 32, 2])
+            if n == 0:
+                nc.vector.tensor_copy(out=dd[:], in_=src)
+            else:
+                nc.scalar.copy(out=dd[:], in_=src)
+            return dd
+
+        def product(n, k, dd):
+            rows = ROWS[k]
+            m = mpool.tile([P, 33 * 128], BF16, name="m", align_bytes=64)
+            m6 = m[:].rearrange("p (r q w h l) -> p r q w h l", q=4, w=8, h=2, l=2)
+            d5 = dd[:].rearrange("p r (w q) l -> p r w q l", q=4)
+            b3 = image_view(xbs[k], n)[:, 0 : rows * SIDE].rearrange("p (r z) -> p r z", z=SIDE)
+            for q in range(4):
+                nc.vector.tensor_tensor(
+                    out=m6[:, 0:rows, q],
+                    in0=d5[:, 0:rows, :, q, :].unsqueeze(3).to_broadcast([P, rows, 8, 2, 2]),
+                    in1=b3[:, :, q : q + 32].rearrange("p r (w h l) -> p r w h l", h=2, l=2),
+                    op=mybir.AluOpType.mult,
+                )
+            return m
+
+        w2s = {}
+        tps = {}
+        wgs = {}
+
+        def w_permute(s):
+            k, r, swapped = PASSES[s]
+            w2 = wtmp.tile([P, 2, 4, P], BF16, name="w2")
+            for h in range(2):
+                wv = w_sb[:, h, :].rearrange("p (c i a j t) -> p c i a j t", c=16, i=4, a=4, j=4, t=4)
+                dst = w2[:, h].rearrange("p t (c a v) -> p t c a v", a=4, v=2)
+                for v in range(2):
+                    al, be = SETS[k][v]
+                    if swapped:
+                        src = wv[:, :, r + be, :, r + al, :].rearrange("p c t a -> p t c a")
+                    else:
+                        src = wv[:, :, r + al, :, r + be, :].rearrange("p c a t -> p t c a")
+                    nc.scalar.copy(out=dst[:, :, :, :, v], in_=src)
+            w2s[s] = w2
+
+        def w_transpose(s):
+            tp = banks.tile([P, 4, 2, P], BF16, name="tp", tag="bank")
+            for t in range(4):
+                for h in range(2):
+                    nc.tensor.transpose(tp[:, t, h, :], w2s[s][:, h, t, :], ident[:])
+            tps[s] = tp
+
+        def w_copy_out(s):
+            wg = wtmp.tile([P, 1024], BF16, name="wg", align_bytes=64)
+            nc.scalar.copy(
+                out=wg[:].rearrange("p (h o t) -> p h o t", h=2, t=4),
+                in_=tps[s][:].rearrange("p t h o -> p h o t"),
+            )
+            wgs[s] = wg
+
+        def w_quantise(s):
+            nc.vector.quantize_mx(
+                out=wc[:, s * 256 : (s + 1) * 256].bitcast(FP8X4),
+                scales=ws[:, s * 256 : (s + 1) * 256],
+                in_=wgs[s][:],
+            )
+
+        def quantise(m, r):
+            codes = ring.tile([P, 1024], U32, name="codes", align_bytes=64)
+            scales = ring.tile([P, 1024], U8, name="scales", align_bytes=64)
+            nc.vector.quantize_mx(
+                out=codes[:].bitcast(FP8X4),
+                scales=scales[:],
+                in_=m[:, r * 128 : r * 128 + 4096],
+            )
+            return codes, scales
+
+        def multiply(s, acc, codes, scales):
+            for j in range(2):
+                for h in range(2):
+                    lo = s * 256 + h * 128
+                    nc.tensor.matmul_mx(
+                        out=acc[(j, h)][:],
+                        lhsT=wc[:, lo : lo + 128].bitcast(FP8X4),
+                        lhsT_scale=ws[:, lo : lo + 128],
+                        rhs=codes[:, j * 512 : (j + 1) * 512].bitcast(FP8X4),
+                        rhs_scale=scales[:, j * 512 : (j + 1) * 512],
+                        start=(s == 0),
+                        stop=(s == 7),
+                    )
+
+        def new_acc():
+            acc = {}
+            for j in range(2):
+                for h in range(2):
+                    acc[(j, h)] = banks.tile([P, 512], F32, name="acc", tag="bank")
+            return acc
+
+        def store(n, acc):
+            for j in range(2):
+                for h in range(2):
+                    res = outpool.tile([P, 512], F32, name="res")
+                    dst = res[:].rearrange("p (y w q) -> p y w q", w=8, q=4)
+                    src = acc[(j, h)][:].rearrange("p (y q w) -> p y w q", q=4, w=8)
+                    if n == NIMG - 1 and h == 1:
+                        nc.vector.tensor_copy(out=dst, in_=src)
+                    else:
+                        nc.scalar.copy(out=dst, in_=src)
+                    nc.sync.dma_start(
+                        out=out[n, h * 128 : (h + 1) * 128, j * 16 : (j + 1) * 16, :].rearrange("o y z -> o (y z)"),
+                        in_=res[:],
+                    )
+
+        units = [(n, k) for n in range(NIMG) for k in range(3)]
+        pairs = {0: ((0, 1),), 1: ((2, 3), (4, 5)), 2: ((6, 7),)}
+        steps = [("P", 0, 0)]
+        for i, (n, k) in enumerate(units):
+            if i + 1 < len(units):
+                steps.append(("P", units[i + 1][0], units[i + 1][1]))
+            for pr in pairs[k]:
+                steps.append(("Q", n, pr))
+
+        dds = {0: make_dd(0)}
+        maps = {}
+        accs = {}
+        quantised = {}
+
+        def multiply_image_pass(n, s):
+            if s == 0:
+                accs[n] = new_acc()
+            codes, scales = quantised[(n, s)]
+            multiply(s, accs[n], codes, scales)
+            if s == 7:
+                store(n, accs[n])
+
+        w_permute(0)
+        w_transpose(0)
+        w_permute(1)
+        w_transpose(1)
+        w_copy_out(0)
+        dds[1] = make_dd(1)
+        w_permute(2)
+        w_transpose(2)
+        w_copy_out(1)
+        w_permute(3)
+        w_transpose(3)
+        w_copy_out(2)
+
+        FIRST_W_STEP = 7
+        for i, step in enumerate(steps):
+            if step[0] == "P":
+                maps[(step[1], step[2])] = product(step[1], step[2], dds[step[1]])
+            else:
+                n = step[1]
+                for s in step[2]:
+                    quantised[(n, s)] = quantise(maps[(n, PASSES[s][0])], PASSES[s][1])
+                if n >= 2:
+                    for s in step[2]:
+                        multiply_image_pass(n, s)
+            s = i - FIRST_W_STEP
+            if 0 <= s < 8:
+                w_quantise(s)
+                if s < 7:
+                    multiply_image_pass(0, s)
+                if s + 4 < 8:
+                    w_permute(s + 4)
+                    w_transpose(s + 4)
+                if s + 3 < 8:
+                    w_copy_out(s + 3)
+                if s == 1:
+                    dds[2] = make_dd(2)
+                if s == 7:
+                    multiply_image_pass(0, 7)
+                    dds[3] = make_dd(3)
+                    for s1 in range(8):
+                        multiply_image_pass(1, s1)

@@ -44,6 +44,8 @@ def tile_fast2order_de_conv_kernel(tc, x, W, out):
 
         ident = const.tile([P, P], BF16, name="ident")
         make_identity(nc, ident[:])
+        ident32 = const.tile([P, P], F32, name="ident32")
+        make_identity(nc, ident32[:])
 
         x_cn = x.rearrange("n c h w -> c n (h w)")
         GROUPS = ((0, 1), (1, NIMG))
@@ -116,34 +118,43 @@ def tile_fast2order_de_conv_kernel(tc, x, W, out):
         tps = {}
         wgs = {}
 
+        w16 = w_sb[:].rearrange("p h (c i a j t) -> p (h c) i a j t", c=16, i=4, a=4, j=4, t=4)
+        w32 = w_sb[:].bitcast(F32).rearrange("p h (c i a j u) -> p (h c) i a j u", c=16, i=4, a=4, j=4, u=2)
+
         def w_permute(s):
             k, r, swapped = PASSES[s]
-            w2 = wtmp.tile([P, 2, 4, P], BF16, name="w2")
-            for h in range(2):
-                wv = w_sb[:, h, :].rearrange("p (c i a j t) -> p c i a j t", c=16, i=4, a=4, j=4, t=4)
-                dst = w2[:, h].rearrange("p t (c a v) -> p t c a v", a=4, v=2)
-                for v in range(2):
-                    al, be = SETS[k][v]
-                    if swapped:
-                        src = wv[:, :, r + be, :, r + al, :].rearrange("p c t a -> p t c a")
-                    else:
-                        src = wv[:, :, r + al, :, r + be, :].rearrange("p c a t -> p t c a")
-                    nc.scalar.copy(out=dst[:, :, :, :, v], in_=src)
+            if swapped:
+                w2 = wtmp.tile([P, 4, 2, P], BF16, name="w2")
+            else:
+                w2 = wtmp.tile([P, 2, 2, P], F32, name="w2w")
+            dst = w2[:].rearrange("p t h (c a v) -> p t (h c) a v", a=4, v=2)
+            for v in range(2):
+                al, be = SETS[k][v]
+                if swapped:
+                    src = w16[:, :, r + be, :, r + al, :].rearrange("p g t a -> p t g a")
+                else:
+                    src = w32[:, :, r + al, :, r + be, :].rearrange("p g a u -> p u g a")
+                nc.scalar.copy(out=dst[:, :, :, :, v], in_=src)
             w2s[s] = w2
 
         def w_transpose(s):
-            tp = banks.tile([P, 4, 2, P], BF16, name="tp", tag="bank")
-            for t in range(4):
+            swapped = PASSES[s][2]
+            if swapped:
+                tp = banks.tile([P, 4, 2, P], BF16, name="tp", tag="bank")
+            else:
+                tp = banks.tile([P, 2, 2, P], F32, name="tpw", tag="bank")
+            for t in range(4 if swapped else 2):
                 for h in range(2):
-                    nc.tensor.transpose(tp[:, t, h, :], w2s[s][:, h, t, :], ident[:])
+                    nc.tensor.transpose(tp[:, t, h, :], w2s[s][:, t, h, :], ident[:] if swapped else ident32[:])
             tps[s] = tp
 
         def w_copy_out(s):
             wg = wtmp.tile([P, 1024], BF16, name="wg", align_bytes=64)
-            nc.scalar.copy(
-                out=wg[:].rearrange("p (h o t) -> p h o t", h=2, t=4),
-                in_=tps[s][:].rearrange("p t h o -> p h o t"),
-            )
+            if PASSES[s][2]:
+                dst = wg[:].rearrange("p (h o t) -> p h o t", h=2, t=4)
+            else:
+                dst = wg[:].bitcast(F32).rearrange("p (h o t) -> p h o t", h=2, t=2)
+            nc.scalar.copy(out=dst, in_=tps[s][:].rearrange("p t h o -> p h o t"))
             wgs[s] = wg
 
         def w_quantise(s):
@@ -153,29 +164,31 @@ def tile_fast2order_de_conv_kernel(tc, x, W, out):
                 in_=wgs[s][:],
             )
 
-        def quantise(m, r):
-            codes = ring.tile([P, 1024], U32, name="codes", align_bytes=64)
-            scales = ring.tile([P, 1024], U8, name="scales", align_bytes=64)
+        def quantise(m, r, j=None):
+            cols = 1024 if j is None else 512
+            first = r * 128 + (0 if j is None else j * 2048)
+            kind = "" if j is None else "_half"
+            codes = ring.tile([P, cols], U32, name="codes" + kind, align_bytes=64, bufs=16 if j is None else 4)
+            scales = ring.tile([P, cols], U8, name="scales" + kind, align_bytes=64, bufs=16 if j is None else 4)
             nc.vector.quantize_mx(
                 out=codes[:].bitcast(FP8X4),
                 scales=scales[:],
-                in_=m[:, r * 128 : r * 128 + 4096],
+                in_=m[:, first : first + 4 * cols],
             )
             return codes, scales
 
-        def multiply(s, acc, codes, scales):
-            for j in range(2):
-                for h in range(2):
-                    lo = s * 256 + h * 128
-                    nc.tensor.matmul_mx(
-                        out=acc[(j, h)][:],
-                        lhsT=wc[:, lo : lo + 128].bitcast(FP8X4),
-                        lhsT_scale=ws[:, lo : lo + 128],
-                        rhs=codes[:, j * 512 : (j + 1) * 512].bitcast(FP8X4),
-                        rhs_scale=scales[:, j * 512 : (j + 1) * 512],
-                        start=(s == 0),
-                        stop=(s == 7),
-                    )
+        def multiply(s, acc, codes, scales, j, at):
+            for h in range(2):
+                lo = s * 256 + h * 128
+                nc.tensor.matmul_mx(
+                    out=acc[(j, h)][:],
+                    lhsT=wc[:, lo : lo + 128].bitcast(FP8X4),
+                    lhsT_scale=ws[:, lo : lo + 128],
+                    rhs=codes[:, at : at + 512].bitcast(FP8X4),
+                    rhs_scale=scales[:, at : at + 512],
+                    start=(s == 0),
+                    stop=(s == 7),
+                )
 
         def new_acc():
             acc = {}
@@ -184,20 +197,19 @@ def tile_fast2order_de_conv_kernel(tc, x, W, out):
                     acc[(j, h)] = banks.tile([P, 512], F32, name="acc", tag="bank")
             return acc
 
-        def store(n, acc):
-            for j in range(2):
-                for h in range(2):
-                    res = outpool.tile([P, 512], F32, name="res")
-                    dst = res[:].rearrange("p (y w q) -> p y w q", w=8, q=4)
-                    src = acc[(j, h)][:].rearrange("p (y q w) -> p y w q", q=4, w=8)
-                    if n == NIMG - 1 and h == 1:
-                        nc.vector.tensor_copy(out=dst, in_=src)
-                    else:
-                        nc.scalar.copy(out=dst, in_=src)
-                    nc.sync.dma_start(
-                        out=out[n, h * 128 : (h + 1) * 128, j * 16 : (j + 1) * 16, :].rearrange("o y z -> o (y z)"),
-                        in_=res[:],
-                    )
+        def store(n, acc, j):
+            for h in range(2):
+                res = outpool.tile([P, 512], F32, name="res")
+                dst = res[:].rearrange("p (y w q) -> p y w q", w=8, q=4)
+                src = acc[(j, h)][:].rearrange("p (y q w) -> p y w q", q=4, w=8)
+                if n == NIMG - 1 and j == 1 and h == 1:
+                    nc.vector.tensor_copy(out=dst, in_=src)
+                else:
+                    nc.scalar.copy(out=dst, in_=src)
+                nc.sync.dma_start(
+                    out=out[n, h * 128 : (h + 1) * 128, j * 16 : (j + 1) * 16, :].rearrange("o y z -> o (y z)"),
+                    in_=res[:],
+                )
 
         units = [(n, k) for n in range(NIMG) for k in range(3)]
         pairs = {0: ((0, 1),), 1: ((2, 3), (4, 5)), 2: ((6, 7),)}
@@ -217,9 +229,11 @@ def tile_fast2order_de_conv_kernel(tc, x, W, out):
             if s == 0:
                 accs[n] = new_acc()
             codes, scales = quantised[(n, s)]
-            multiply(s, accs[n], codes, scales)
+            for j in range(2):
+                multiply(s, accs[n], codes, scales, j, j * 512)
             if s == 7:
-                store(n, accs[n])
+                for j in range(2):
+                    store(n, accs[n], j)
 
         w_permute(0)
         w_transpose(0)
@@ -238,6 +252,13 @@ def tile_fast2order_de_conv_kernel(tc, x, W, out):
         for i, step in enumerate(steps):
             if step[0] == "P":
                 maps[(step[1], step[2])] = product(step[1], step[2], dds[step[1]])
+            elif step[1] == NIMG - 1 and step[2] == (6, 7):
+                n = step[1]
+                for j in range(2):
+                    for s in step[2]:
+                        codes, scales = quantise(maps[(n, PASSES[s][0])], PASSES[s][1], j)
+                        multiply(s, accs[n], codes, scales, j, 0)
+                    store(n, accs[n], j)
             else:
                 n = step[1]
                 for s in step[2]:

@@ -42,6 +42,15 @@ def tile_fast2order_de_conv_kernel(tc, x, W, out):
         banks = ctx.enter_context(tc.psum_pool(name="banks", bufs=8))
         ctx.enter_context(tc.manual_schedule())
 
+        w_sb = const.tile([P, 2, 4096], BF16, name="w_sb")
+        w_view = W.rearrange("(h o) f -> o h f", h=2)
+        for h in range(2):
+            for half in range(2):
+                nc.gpsimd.dma_start(
+                    out=w_sb[:, h, half * 2048 : (half + 1) * 2048],
+                    in_=w_view[:, h, half * 2048 : (half + 1) * 2048],
+                )
+
         ident = const.tile([P, P], BF16, name="ident")
         make_identity(nc, ident[:])
         ident32 = const.tile([P, P], F32, name="ident32")
@@ -77,10 +86,6 @@ def tile_fast2order_de_conv_kernel(tc, x, W, out):
         load_xa(0)
         load_xb(0, 0)
         load_xb(1, 0)
-        w_sb = const.tile([P, 2, 4096], BF16, name="w_sb")
-        w_view = W.rearrange("(h o) f -> o h f", h=2)
-        for h in range(2):
-            nc.sync.dma_start(out=w_sb[:, h, :], in_=w_view[:, h, :])
         load_xb(2, 0)
         load_xa(1)
         for k in range(3):

@@ -95,26 +95,29 @@ def tile_fast2order_de_conv_kernel(tc, x, W, out):
         ws = const.tile([P, 2048], U8, name="ws", align_bytes=64)
 
         def make_dd(n):
-            dd = ddpool.tile([P, 33, 32, 2], BF16, name="dd")
             src = image_view(xa, n)[:, 0 : 33 * SIDE].rearrange("p (r z) -> p r z", z=SIDE)[:, :, 0:32]
-            src = src.unsqueeze(3).to_broadcast([P, 33, 32, 2])
-            if n == 0:
-                nc.vector.tensor_copy(out=dd[:], in_=src)
-            else:
-                nc.scalar.copy(out=dd[:], in_=src)
-            return dd
+            src = src.rearrange("p r (w q) -> p r w q", q=4)
+            tiles = []
+            for q in range(4):
+                ea = ddpool.tile([P, 33, 8, 4], BF16, name="ea%d" % q)
+                one = src[:, :, :, q : q + 1].to_broadcast([P, 33, 8, 4])
+                if n == 0 and q < 2:
+                    nc.vector.tensor_copy(out=ea[:], in_=one)
+                else:
+                    nc.scalar.copy(out=ea[:], in_=one)
+                tiles.append(ea)
+            return tiles
 
         def product(n, k, dd):
             rows = ROWS[k]
             m = mpool.tile([P, 33 * 128], BF16, name="m", align_bytes=64)
-            m6 = m[:].rearrange("p (r q w h l) -> p r q w h l", q=4, w=8, h=2, l=2)
-            d5 = dd[:].rearrange("p r (w q) l -> p r w q l", q=4)
+            m4 = m[:].rearrange("p (r q e) -> p r q e", q=4, e=32)
             b3 = image_view(xbs[k], n)[:, 0 : rows * SIDE].rearrange("p (r z) -> p r z", z=SIDE)
             for q in range(4):
                 nc.vector.tensor_tensor(
-                    out=m6[:, 0:rows, q],
-                    in0=d5[:, 0:rows, :, q, :].unsqueeze(3).to_broadcast([P, rows, 8, 2, 2]),
-                    in1=b3[:, :, q : q + 32].rearrange("p r (w h l) -> p r w h l", h=2, l=2),
+                    out=m4[:, 0:rows, q, :],
+                    in0=dd[q][:, 0:rows].rearrange("p r w t -> p r (w t)"),
+                    in1=b3[:, :, q : q + 32],
                     op=mybir.AluOpType.mult,
                 )
             return m

@@ -12,12 +12,15 @@ U8 = mybir.dt.uint8
 FP8X4 = mybir.dt.float8_e4m3fn_x4
 
 P = 128
-NIMG = 4
+IMAGES = 4
 SIDE = 35
-PIX = SIDE * SIDE
-XPITCH = 1168
-SETS = (((0, 0), (2, 2)), ((0, 1), (2, 0)), ((0, 3), (2, 3)))
-ROWS = (33, 33, 32)
+GRID = 32
+ROW = 4 * GRID
+X_PITCH = 1168
+
+FIRST_ROW = (0, 2)
+SECOND_ROW = ((0, 2), (1, 0), (3, 3))
+MAP_ROWS = (33, 33, 32)
 PASSES = (
     (0, 0, False),
     (0, 1, False),
@@ -28,266 +31,266 @@ PASSES = (
     (2, 0, False),
     (2, 0, True),
 )
+PASS_PAIRS = (((0, 1),), ((2, 3), (4, 5)), ((6, 7),))
+LAST = len(PASSES) - 1
+IMAGE_GROUPS = ((0, 1), (1, IMAGES))
+RING = 16
+FIRST_W_STEP = 7
+W_AHEAD = 4
+
+
+def vector_steps():
+    units = [(n, k) for n in range(IMAGES) for k in range(3)]
+    steps = [("product", 0, 0)]
+    for index, (n, k) in enumerate(units):
+        if index + 1 < len(units):
+            steps.append(("product", units[index + 1][0], units[index + 1][1]))
+        for pair in PASS_PAIRS[k]:
+            steps.append(("quantise", n, pair))
+    return steps
 
 
 def tile_fast2order_de_conv_kernel(tc, x, W, out):
     nc = tc.nc
     with ExitStack() as ctx:
-        const = ctx.enter_context(tc.tile_pool(name="const", bufs=1))
-        ddpool = ctx.enter_context(tc.tile_pool(name="ddpool", bufs=2))
-        mpool = ctx.enter_context(tc.tile_pool(name="mpool", bufs=3))
-        ring = ctx.enter_context(tc.tile_pool(name="ring", bufs=16))
-        wtmp = ctx.enter_context(tc.tile_pool(name="wtmp", bufs=4))
-        outpool = ctx.enter_context(tc.tile_pool(name="outpool", bufs=4))
+        resident = ctx.enter_context(tc.tile_pool(name="resident", bufs=1))
+        repeated_pool = ctx.enter_context(tc.tile_pool(name="repeated", bufs=2))
+        map_pool = ctx.enter_context(tc.tile_pool(name="maps", bufs=3))
+        ring = ctx.enter_context(tc.tile_pool(name="ring", bufs=RING))
+        w_stage = ctx.enter_context(tc.tile_pool(name="w_stage", bufs=W_AHEAD))
+        result_pool = ctx.enter_context(tc.tile_pool(name="results", bufs=4))
         banks = ctx.enter_context(tc.psum_pool(name="banks", bufs=8))
         ctx.enter_context(tc.manual_schedule())
 
-        w_sb = const.tile([P, 2, 4096], BF16, name="w_sb")
+        w_rows = resident.tile([P, 2, 4096], BF16, name="w_rows")
         w_view = W.rearrange("(h o) f -> o h f", h=2)
         for h in range(2):
             for half in range(2):
                 nc.gpsimd.dma_start(
-                    out=w_sb[:, h, half * 2048 : (half + 1) * 2048],
+                    out=w_rows[:, h, half * 2048 : (half + 1) * 2048],
                     in_=w_view[:, h, half * 2048 : (half + 1) * 2048],
                 )
 
-        ident = const.tile([P, P], BF16, name="ident")
-        make_identity(nc, ident[:])
-        ident32 = const.tile([P, P], F32, name="ident32")
-        make_identity(nc, ident32[:])
+        ident_bf16 = resident.tile([P, P], BF16, name="ident_bf16")
+        make_identity(nc, ident_bf16[:])
+        ident_f32 = resident.tile([P, P], F32, name="ident_f32")
+        make_identity(nc, ident_f32[:])
 
         x_cn = x.rearrange("n c h w -> c n (h w)")
-        GROUPS = ((0, 1), (1, NIMG))
-        xa = [const.tile([P, n1 - n0, XPITCH], BF16, name="xa_%d" % n0) for (n0, n1) in GROUPS]
-        xbs = [
-            [const.tile([P, n1 - n0, XPITCH], BF16, name="xb%d_%d" % (k, n0)) for (n0, n1) in GROUPS]
+        first = [
+            resident.tile([P, n1 - n0, X_PITCH], BF16, name="first_%d" % n0) for (n0, n1) in IMAGE_GROUPS
+        ]
+        second = [
+            [resident.tile([P, n1 - n0, X_PITCH], BF16, name="second%d_%d" % (k, n0)) for (n0, n1) in IMAGE_GROUPS]
             for k in range(3)
         ]
 
         def load_shifted(tiles, g, length, shift):
-            n0, n1 = GROUPS[g]
+            n0, n1 = IMAGE_GROUPS[g]
             for a in range(4):
                 for v in range(2):
-                    off = shift(a, v)
+                    start = shift(a, v)
                     nc.sync.dma_start(
                         out=tiles[g][2 * a + v : P : 8, :, 0:length],
-                        in_=x_cn[:, n0:n1, off : off + length],
+                        in_=x_cn[:, n0:n1, start : start + length],
                     )
 
-        def load_xa(g):
-            load_shifted(xa, g, 1152, lambda a, v: 2 * SIDE * v + a)
+        def load_first(g):
+            load_shifted(first, g, 33 * SIDE - 3, lambda a, v: SIDE * FIRST_ROW[v] + a)
 
-        def load_xb(k, g):
-            load_shifted(xbs[k], g, ROWS[k] * SIDE, lambda a, v: SIDE * SETS[k][v][1])
+        def load_second(k, g):
+            load_shifted(second[k], g, MAP_ROWS[k] * SIDE, lambda a, v: SIDE * SECOND_ROW[k][v])
 
-        def image_view(tiles, n):
-            return tiles[0][:, 0, :] if n == 0 else tiles[1][:, n - 1, :]
+        def image_rows(tiles, n, rows):
+            flat = tiles[0][:, 0, :] if n == 0 else tiles[1][:, n - 1, :]
+            return flat[:, 0 : rows * SIDE].rearrange("p (r z) -> p r z", z=SIDE)
 
-        load_xa(0)
-        load_xb(0, 0)
-        load_xb(1, 0)
-        load_xb(2, 0)
-        load_xa(1)
-        for k in range(3):
-            load_xb(k, 1)
+        for g in range(len(IMAGE_GROUPS)):
+            load_first(g)
+            for k in range(3):
+                load_second(k, g)
 
-        wc = const.tile([P, 2048], U32, name="wc", align_bytes=64)
-        ws = const.tile([P, 2048], U8, name="ws", align_bytes=64)
+        w_codes = resident.tile([P, 2048], U32, name="w_codes", align_bytes=64)
+        w_scales = resident.tile([P, 2048], U8, name="w_scales", align_bytes=64)
 
-        def make_dd(n):
-            src = image_view(xa, n)[:, 0 : 33 * SIDE].rearrange("p (r z) -> p r z", z=SIDE)[:, :, 0:32]
-            src = src.rearrange("p r (w q) -> p r w q", q=4)
+        def repeat_first_factor(n):
+            columns = image_rows(first, n, 33)[:, :, 0:GRID].rearrange("p r (w q) -> p r w q", q=4)
             tiles = []
             for q in range(4):
-                ea = ddpool.tile([P, 33, 8, 4], BF16, name="ea%d" % q)
-                one = src[:, :, :, q : q + 1].to_broadcast([P, 33, 8, 4])
+                rep = repeated_pool.tile([P, 33, 8, 4], BF16, name="rep%d" % q)
+                one = columns[:, :, :, q : q + 1].to_broadcast([P, 33, 8, 4])
                 if n == 0 and q < 2:
-                    nc.vector.tensor_copy(out=ea[:], in_=one)
+                    nc.vector.tensor_copy(out=rep[:], in_=one)
                 else:
-                    nc.scalar.copy(out=ea[:], in_=one)
-                tiles.append(ea)
+                    nc.scalar.copy(out=rep[:], in_=one)
+                tiles.append(rep)
             return tiles
 
-        def product(n, k, dd):
-            rows = ROWS[k]
-            m = mpool.tile([P, 33 * 128], BF16, name="m", align_bytes=64)
-            m4 = m[:].rearrange("p (r q e) -> p r q e", q=4, e=32)
-            b3 = image_view(xbs[k], n)[:, 0 : rows * SIDE].rearrange("p (r z) -> p r z", z=SIDE)
+        def product(n, k, rep):
+            rows = MAP_ROWS[k]
+            m = map_pool.tile([P, 33 * ROW], BF16, name="map", align_bytes=64)
+            by_q = m[:].rearrange("p (r q e) -> p r q e", q=4, e=GRID)
+            factor = image_rows(second[k], n, rows)
             for q in range(4):
                 nc.vector.tensor_tensor(
-                    out=m4[:, 0:rows, q, :],
-                    in0=dd[q][:, 0:rows].rearrange("p r w t -> p r (w t)"),
-                    in1=b3[:, :, q : q + 32],
+                    out=by_q[:, 0:rows, q, :],
+                    in0=rep[q][:, 0:rows].rearrange("p r w t -> p r (w t)"),
+                    in1=factor[:, :, q : q + GRID],
                     op=mybir.AluOpType.mult,
                 )
             return m
 
-        w2s = {}
-        tps = {}
-        wgs = {}
-
-        w16 = w_sb[:].rearrange("p h (c i a j t) -> p (h c) i a j t", c=16, i=4, a=4, j=4, t=4)
-        w32 = w_sb[:].bitcast(F32).rearrange("p h (c i a j u) -> p (h c) i a j u", c=16, i=4, a=4, j=4, u=2)
-
-        def w_permute(s):
-            k, r, swapped = PASSES[s]
-            if swapped:
-                w2 = wtmp.tile([P, 4, 2, P], BF16, name="w2")
-            else:
-                w2 = wtmp.tile([P, 2, 2, P], F32, name="w2w")
-            dst = w2[:].rearrange("p t h (c a v) -> p t (h c) a v", a=4, v=2)
-            for v in range(2):
-                al, be = SETS[k][v]
-                if swapped:
-                    src = w16[:, :, r + be, :, r + al, :].rearrange("p g t a -> p t g a")
-                else:
-                    src = w32[:, :, r + al, :, r + be, :].rearrange("p g a u -> p u g a")
-                nc.scalar.copy(out=dst[:, :, :, :, v], in_=src)
-            w2s[s] = w2
-
-        def w_transpose(s):
-            swapped = PASSES[s][2]
-            if swapped:
-                tp = banks.tile([P, 4, 2, P], BF16, name="tp", tag="bank")
-            else:
-                tp = banks.tile([P, 2, 2, P], F32, name="tpw", tag="bank")
-            for t in range(4 if swapped else 2):
-                for h in range(2):
-                    nc.tensor.transpose(tp[:, t, h, :], w2s[s][:, t, h, :], ident[:] if swapped else ident32[:])
-            tps[s] = tp
-
-        def w_copy_out(s):
-            wg = wtmp.tile([P, 1024], BF16, name="wg", align_bytes=64)
-            if PASSES[s][2]:
-                dst = wg[:].rearrange("p (h o t) -> p h o t", h=2, t=4)
-            else:
-                dst = wg[:].bitcast(F32).rearrange("p (h o t) -> p h o t", h=2, t=2)
-            nc.scalar.copy(out=dst, in_=tps[s][:].rearrange("p t h o -> p h o t"))
-            wgs[s] = wg
-
-        def w_quantise(s):
-            nc.vector.quantize_mx(
-                out=wc[:, s * 256 : (s + 1) * 256].bitcast(FP8X4),
-                scales=ws[:, s * 256 : (s + 1) * 256],
-                in_=wgs[s][:],
-            )
-
         def quantise(m, r, j=None):
             cols = 1024 if j is None else 512
-            first = r * 128 + (0 if j is None else j * 2048)
+            start = r * ROW + (0 if j is None else j * 4 * cols)
             kind = "" if j is None else "_half"
-            codes = ring.tile([P, cols], U32, name="codes" + kind, align_bytes=64, bufs=16 if j is None else 4)
-            scales = ring.tile([P, cols], U8, name="scales" + kind, align_bytes=64, bufs=16 if j is None else 4)
+            depth = RING if j is None else 4
+            codes = ring.tile([P, cols], U32, name="codes" + kind, align_bytes=64, bufs=depth)
+            scales = ring.tile([P, cols], U8, name="scales" + kind, align_bytes=64, bufs=depth)
             nc.vector.quantize_mx(
                 out=codes[:].bitcast(FP8X4),
                 scales=scales[:],
-                in_=m[:, first : first + 4 * cols],
+                in_=m[:, start : start + 4 * cols],
             )
             return codes, scales
 
-        def multiply(s, acc, codes, scales, j, at):
+        w_bf16 = w_rows[:].rearrange("p h (c i a j t) -> p (h c) i a j t", c=16, i=4, a=4, j=4, t=4)
+        w_pairs = w_rows[:].bitcast(F32).rearrange("p h (c i a j u) -> p (h c) i a j u", c=16, i=4, a=4, j=4, u=2)
+        sorted_w = {}
+        transposed_w = {}
+        grouped_w = {}
+
+        def sort_w(s):
+            k, r, exchanged = PASSES[s]
+            if exchanged:
+                cols = w_stage.tile([P, 4, 2, P], BF16, name="w_cols")
+            else:
+                cols = w_stage.tile([P, 2, 2, P], F32, name="w_col_pairs")
+            by_v = cols[:].rearrange("p t h (c a v) -> p t (h c) a v", a=4, v=2)
+            for v in range(2):
+                row_a = r + FIRST_ROW[v]
+                row_t = r + SECOND_ROW[k][v]
+                if exchanged:
+                    src = w_bf16[:, :, row_t, :, row_a, :].rearrange("p g t a -> p t g a")
+                else:
+                    src = w_pairs[:, :, row_a, :, row_t, :].rearrange("p g a u -> p u g a")
+                nc.scalar.copy(out=by_v[:, :, :, :, v], in_=src)
+            sorted_w[s] = cols
+
+        def transpose_w(s):
+            exchanged = PASSES[s][2]
+            if exchanged:
+                bank = banks.tile([P, 4, 2, P], BF16, name="w_t", tag="bank")
+            else:
+                bank = banks.tile([P, 2, 2, P], F32, name="w_t_pairs", tag="bank")
+            for t in range(4 if exchanged else 2):
+                for h in range(2):
+                    nc.tensor.transpose(
+                        bank[:, t, h, :], sorted_w[s][:, t, h, :], ident_bf16[:] if exchanged else ident_f32[:]
+                    )
+            transposed_w[s] = bank
+
+        def group_w(s):
+            grouped = w_stage.tile([P, 1024], BF16, name="w_grouped", align_bytes=64)
+            if PASSES[s][2]:
+                dst = grouped[:].rearrange("p (h o t) -> p h o t", h=2, t=4)
+            else:
+                dst = grouped[:].bitcast(F32).rearrange("p (h o t) -> p h o t", h=2, t=2)
+            nc.scalar.copy(out=dst, in_=transposed_w[s][:].rearrange("p t h o -> p h o t"))
+            grouped_w[s] = grouped
+
+        def advance_w(s):
+            if s <= LAST:
+                sort_w(s)
+                transpose_w(s)
+            if 1 <= s <= LAST + 1:
+                group_w(s - 1)
+
+        def quantise_w(s):
+            nc.vector.quantize_mx(
+                out=w_codes[:, s * 256 : (s + 1) * 256].bitcast(FP8X4),
+                scales=w_scales[:, s * 256 : (s + 1) * 256],
+                in_=grouped_w[s][:],
+            )
+
+        def multiply(s, sums, codes, scales, j, at):
             for h in range(2):
-                lo = s * 256 + h * 128
+                lo = s * 256 + h * P
                 nc.tensor.matmul_mx(
-                    out=acc[(j, h)][:],
-                    lhsT=wc[:, lo : lo + 128].bitcast(FP8X4),
-                    lhsT_scale=ws[:, lo : lo + 128],
+                    out=sums[(j, h)][:],
+                    lhsT=w_codes[:, lo : lo + P].bitcast(FP8X4),
+                    lhsT_scale=w_scales[:, lo : lo + P],
                     rhs=codes[:, at : at + 512].bitcast(FP8X4),
                     rhs_scale=scales[:, at : at + 512],
                     start=(s == 0),
-                    stop=(s == 7),
+                    stop=(s == LAST),
                 )
 
-        def new_acc():
-            acc = {}
+        def new_sums():
+            sums = {}
             for j in range(2):
                 for h in range(2):
-                    acc[(j, h)] = banks.tile([P, 512], F32, name="acc", tag="bank")
-            return acc
+                    sums[(j, h)] = banks.tile([P, 512], F32, name="sums", tag="bank")
+            return sums
 
-        def store(n, acc, j):
+        def store(n, sums, j):
             for h in range(2):
-                res = outpool.tile([P, 512], F32, name="res")
+                res = result_pool.tile([P, 512], F32, name="res")
                 dst = res[:].rearrange("p (y w q) -> p y w q", w=8, q=4)
-                src = acc[(j, h)][:].rearrange("p (y q w) -> p y w q", q=4, w=8)
-                if n == NIMG - 1 and j == 1 and h == 1:
+                src = sums[(j, h)][:].rearrange("p (y q w) -> p y w q", q=4, w=8)
+                if n == IMAGES - 1 and j == 1 and h == 1:
                     nc.vector.tensor_copy(out=dst, in_=src)
                 else:
                     nc.scalar.copy(out=dst, in_=src)
                 nc.sync.dma_start(
-                    out=out[n, h * 128 : (h + 1) * 128, j * 16 : (j + 1) * 16, :].rearrange("o y z -> o (y z)"),
+                    out=out[n, h * P : (h + 1) * P, j * 16 : (j + 1) * 16, :].rearrange("o y z -> o (y z)"),
                     in_=res[:],
                 )
 
-        units = [(n, k) for n in range(NIMG) for k in range(3)]
-        pairs = {0: ((0, 1),), 1: ((2, 3), (4, 5)), 2: ((6, 7),)}
-        steps = [("P", 0, 0)]
-        for i, (n, k) in enumerate(units):
-            if i + 1 < len(units):
-                steps.append(("P", units[i + 1][0], units[i + 1][1]))
-            for pr in pairs[k]:
-                steps.append(("Q", n, pr))
-
-        dds = {0: make_dd(0)}
+        repeated = {0: repeat_first_factor(0)}
         maps = {}
-        accs = {}
+        sums_of = {}
         quantised = {}
 
-        def multiply_image_pass(n, s):
+        def multiply_pass(n, s):
             if s == 0:
-                accs[n] = new_acc()
+                sums_of[n] = new_sums()
             codes, scales = quantised[(n, s)]
             for j in range(2):
-                multiply(s, accs[n], codes, scales, j, j * 512)
-            if s == 7:
+                multiply(s, sums_of[n], codes, scales, j, j * 512)
+            if s == LAST:
                 for j in range(2):
-                    store(n, accs[n], j)
+                    store(n, sums_of[n], j)
 
-        w_permute(0)
-        w_transpose(0)
-        w_permute(1)
-        w_transpose(1)
-        w_copy_out(0)
-        dds[1] = make_dd(1)
-        w_permute(2)
-        w_transpose(2)
-        w_copy_out(1)
-        w_permute(3)
-        w_transpose(3)
-        w_copy_out(2)
+        for s in range(W_AHEAD):
+            advance_w(s)
+            if s == 1:
+                repeated[1] = repeat_first_factor(1)
 
-        FIRST_W_STEP = 7
-        for i, step in enumerate(steps):
-            if step[0] == "P":
-                maps[(step[1], step[2])] = product(step[1], step[2], dds[step[1]])
-            elif step[1] == NIMG - 1 and step[2] == (6, 7):
-                n = step[1]
+        for index, step in enumerate(vector_steps()):
+            n = step[1]
+            if step[0] == "product":
+                maps[(n, step[2])] = product(n, step[2], repeated[n])
+            elif n == IMAGES - 1 and step[2] == PASS_PAIRS[2][0]:
                 for j in range(2):
                     for s in step[2]:
                         codes, scales = quantise(maps[(n, PASSES[s][0])], PASSES[s][1], j)
-                        multiply(s, accs[n], codes, scales, j, 0)
-                    store(n, accs[n], j)
+                        multiply(s, sums_of[n], codes, scales, j, 0)
+                    store(n, sums_of[n], j)
             else:
-                n = step[1]
                 for s in step[2]:
                     quantised[(n, s)] = quantise(maps[(n, PASSES[s][0])], PASSES[s][1])
                 if n >= 2:
                     for s in step[2]:
-                        multiply_image_pass(n, s)
-            s = i - FIRST_W_STEP
-            if 0 <= s < 8:
-                w_quantise(s)
-                if s < 7:
-                    multiply_image_pass(0, s)
-                if s + 4 < 8:
-                    w_permute(s + 4)
-                    w_transpose(s + 4)
-                if s + 3 < 8:
-                    w_copy_out(s + 3)
+                        multiply_pass(n, s)
+            s = index - FIRST_W_STEP
+            if 0 <= s <= LAST:
+                quantise_w(s)
+                multiply_pass(0, s)
+                advance_w(s + W_AHEAD)
                 if s == 1:
-                    dds[2] = make_dd(2)
-                if s == 7:
-                    multiply_image_pass(0, 7)
-                    dds[3] = make_dd(3)
-                    for s1 in range(8):
-                        multiply_image_pass(1, s1)
+                    repeated[2] = repeat_first_factor(2)
+                if s == LAST:
+                    repeated[3] = repeat_first_factor(3)
+                    for s1 in range(LAST + 1):
+                        multiply_pass(1, s1)

@@ -16,37 +16,36 @@ IMAGES = 4
 SIDE = 35
 GRID = 32
 ROW = 4 * GRID
-X_PITCH = 1168
+X_PITCH = 1232
 
-FIRST_ROW = (0, 2)
-SECOND_ROW = ((0, 2), (1, 0), (3, 3))
-MAP_ROWS = (33, 33, 32)
+SAME, NEAR, FAR = range(3)
+MAP_ROWS = 35
+DISTANCE = ((0, 3), (1, 2))
+PRODUCT_ROWS = (35, 34)
 PASSES = (
-    (0, 0, False),
-    (0, 1, False),
-    (1, 0, False),
-    (1, 0, True),
-    (1, 1, False),
-    (1, 1, True),
-    (2, 0, False),
-    (2, 0, True),
+    (NEAR, 0, False),
+    (NEAR, 0, True),
+    (NEAR, 1, False),
+    (NEAR, 1, True),
+    (FAR, 0, False),
+    (FAR, 0, True),
+    (SAME, 0, False),
+    (SAME, 1, False),
 )
-PASS_PAIRS = (((0, 1),), ((2, 3), (4, 5)), ((6, 7),))
 LAST = len(PASSES) - 1
 IMAGE_GROUPS = ((0, 1), (1, IMAGES))
-RING = 16
-FIRST_W_STEP = 7
+RING = 14
+FIRST_W_STEP = 6
 W_AHEAD = 4
 
 
 def vector_steps():
-    units = [(n, k) for n in range(IMAGES) for k in range(3)]
-    steps = [("product", 0, 0)]
-    for index, (n, k) in enumerate(units):
-        if index + 1 < len(units):
-            steps.append(("product", units[index + 1][0], units[index + 1][1]))
-        for pair in PASS_PAIRS[k]:
-            steps.append(("quantise", n, pair))
+    steps = [("product", 0, 1), ("product", 0, 0)]
+    for n in range(IMAGES):
+        steps += [("quantise", n, (0, 1)), ("quantise", n, (2, 3))]
+        if n + 1 < IMAGES:
+            steps += [("product", n + 1, 0), ("product", n + 1, 1)]
+        steps += [("quantise", n, (4, 5)), ("quantise", n, (6, 7))]
     return steps
 
 
@@ -55,7 +54,7 @@ def tile_fast2order_de_conv_kernel(tc, x, W, out):
     with ExitStack() as ctx:
         resident = ctx.enter_context(tc.tile_pool(name="resident", bufs=1))
         repeated_pool = ctx.enter_context(tc.tile_pool(name="repeated", bufs=2))
-        map_pool = ctx.enter_context(tc.tile_pool(name="maps", bufs=3))
+        map_pool = ctx.enter_context(tc.tile_pool(name="maps", bufs=2))
         ring = ctx.enter_context(tc.tile_pool(name="ring", bufs=RING))
         w_stage = ctx.enter_context(tc.tile_pool(name="w_stage", bufs=W_AHEAD))
         result_pool = ctx.enter_context(tc.tile_pool(name="results", bufs=4))
@@ -82,8 +81,12 @@ def tile_fast2order_de_conv_kernel(tc, x, W, out):
         ]
         second = [
             [resident.tile([P, n1 - n0, X_PITCH], BF16, name="second%d_%d" % (k, n0)) for (n0, n1) in IMAGE_GROUPS]
-            for k in range(3)
+            for k in range(2)
         ]
+        for g in range(len(IMAGE_GROUPS)):
+            for k in range(2):
+                unused = (SIDE - DISTANCE[k][1]) * SIDE // 16 * 16
+                nc.vector.memset(second[k][g][:, :, unused:X_PITCH], 0.0)
 
         def load_shifted(tiles, g, length, shift):
             n0, n1 = IMAGE_GROUPS[g]
@@ -91,15 +94,20 @@ def tile_fast2order_de_conv_kernel(tc, x, W, out):
                 for v in range(2):
                     start = shift(a, v)
                     nc.sync.dma_start(
-                        out=tiles[g][2 * a + v : P : 8, :, 0:length],
-                        in_=x_cn[:, n0:n1, start : start + length],
+                        out=tiles[g][2 * a + v : P : 8, :, 0 : length(v)],
+                        in_=x_cn[:, n0:n1, start : start + length(v)],
                     )
 
         def load_first(g):
-            load_shifted(first, g, 33 * SIDE - 3, lambda a, v: SIDE * FIRST_ROW[v] + a)
+            load_shifted(first, g, lambda v: SIDE * SIDE - 3, lambda a, v: a)
 
         def load_second(k, g):
-            load_shifted(second[k], g, MAP_ROWS[k] * SIDE, lambda a, v: SIDE * SECOND_ROW[k][v])
+            load_shifted(
+                second[k],
+                g,
+                lambda v: min(PRODUCT_ROWS[k], SIDE - DISTANCE[k][v]) * SIDE,
+                lambda a, v: SIDE * DISTANCE[k][v],
+            )
 
         def image_rows(tiles, n, rows):
             flat = tiles[0][:, 0, :] if n == 0 else tiles[1][:, n - 1, :]
@@ -107,18 +115,18 @@ def tile_fast2order_de_conv_kernel(tc, x, W, out):
 
         for g in range(len(IMAGE_GROUPS)):
             load_first(g)
-            for k in range(3):
-                load_second(k, g)
+            load_second(1, g)
+            load_second(0, g)
 
         w_codes = resident.tile([P, 2048], U32, name="w_codes", align_bytes=64)
         w_scales = resident.tile([P, 2048], U8, name="w_scales", align_bytes=64)
 
         def repeat_first_factor(n):
-            columns = image_rows(first, n, 33)[:, :, 0:GRID].rearrange("p r (w q) -> p r w q", q=4)
+            columns = image_rows(first, n, MAP_ROWS)[:, :, 0:GRID].rearrange("p r (w q) -> p r w q", q=4)
             tiles = []
             for q in range(4):
-                rep = repeated_pool.tile([P, 33, 8, 4], BF16, name="rep%d" % q)
-                one = columns[:, :, :, q : q + 1].to_broadcast([P, 33, 8, 4])
+                rep = repeated_pool.tile([P, MAP_ROWS, 8, 4], BF16, name="rep%d" % q)
+                one = columns[:, :, :, q : q + 1].to_broadcast([P, MAP_ROWS, 8, 4])
                 if n == 0 and q < 2:
                     nc.vector.tensor_copy(out=rep[:], in_=one)
                 else:
@@ -127,8 +135,11 @@ def tile_fast2order_de_conv_kernel(tc, x, W, out):
             return tiles
 
         def product(n, k, rep):
-            rows = MAP_ROWS[k]
-            m = map_pool.tile([P, 33 * ROW], BF16, name="map", align_bytes=64)
+            rows = PRODUCT_ROWS[k]
+            if k == 0:
+                m = map_pool.tile([P, MAP_ROWS * ROW], BF16, name="same", align_bytes=64)
+            else:
+                m = map_pool.tile([P, MAP_ROWS * ROW], BF16, name="near", align_bytes=64, bufs=1)
             by_q = m[:].rearrange("p (r q e) -> p r q e", q=4, e=GRID)
             factor = image_rows(second[k], n, rows)
             for q in range(4):
@@ -139,6 +150,15 @@ def tile_fast2order_de_conv_kernel(tc, x, W, out):
                     op=mybir.AluOpType.mult,
                 )
             return m
+
+        def carry(to, to_v, to_row, source, from_v, from_row, rows):
+            nc.sync.dma_start(
+                out=to[to_v:P:2, to_row * ROW : (to_row + rows) * ROW],
+                in_=source[from_v:P:2, from_row * ROW : (from_row + rows) * ROW],
+            )
+
+        def far_map():
+            return map_pool.tile([P, MAP_ROWS * ROW], BF16, name="far", align_bytes=64)
 
         def quantise(m, r, j=None):
             cols = 1024 if j is None else 512
@@ -161,20 +181,29 @@ def tile_fast2order_de_conv_kernel(tc, x, W, out):
         grouped_w = {}
 
         def sort_w(s):
-            k, r, exchanged = PASSES[s]
+            m, r, exchanged = PASSES[s]
             if exchanged:
                 cols = w_stage.tile([P, 4, 2, P], BF16, name="w_cols")
             else:
                 cols = w_stage.tile([P, 2, 2, P], F32, name="w_col_pairs")
             by_v = cols[:].rearrange("p t h (c a v) -> p t (h c) a v", a=4, v=2)
-            for v in range(2):
-                row_a = r + FIRST_ROW[v]
-                row_t = r + SECOND_ROW[k][v]
-                if exchanged:
-                    src = w_bf16[:, :, row_t, :, row_a, :].rearrange("p g t a -> p t g a")
+            if m == SAME:
+                for v in range(2):
+                    row = r + 2 * v
+                    src = w_pairs[:, :, row, :, row, :].rearrange("p g a u -> p u g a")
+                    nc.scalar.copy(out=by_v[:, :, :, :, v], in_=src)
+            else:
+                if m == NEAR:
+                    row_a, row_t = r, slice(r + 1, r + 3)
                 else:
-                    src = w_pairs[:, :, row_a, :, row_t, :].rearrange("p g a u -> p u g a")
-                nc.scalar.copy(out=by_v[:, :, :, :, v], in_=src)
+                    row_a, row_t = slice(0, 3, 2), 3
+                if exchanged:
+                    src = w_bf16[:, :, row_t, :, row_a, :]
+                    src = src.rearrange("p g v t a -> p t g a v" if m == NEAR else "p g t v a -> p t g a v")
+                else:
+                    src = w_pairs[:, :, row_a, :, row_t, :]
+                    src = src.rearrange("p g a v u -> p u g a v" if m == NEAR else "p g v a u -> p u g a v")
+                nc.scalar.copy(out=by_v, in_=src)
             sorted_w[s] = cols
 
         def transpose_w(s):
@@ -242,7 +271,7 @@ def tile_fast2order_de_conv_kernel(tc, x, W, out):
                     nc.vector.tensor_copy(out=dst, in_=src)
                 else:
                     nc.scalar.copy(out=dst, in_=src)
-                nc.sync.dma_start(
+                nc.scalar.dma_start(
                     out=out[n, h * P : (h + 1) * P, j * 16 : (j + 1) * 16, :].rearrange("o y z -> o (y z)"),
                     in_=res[:],
                 )
@@ -264,14 +293,25 @@ def tile_fast2order_de_conv_kernel(tc, x, W, out):
 
         for s in range(W_AHEAD):
             advance_w(s)
-            if s == 1:
+            if s == 0:
                 repeated[1] = repeat_first_factor(1)
 
         for index, step in enumerate(vector_steps()):
             n = step[1]
             if step[0] == "product":
-                maps[(n, step[2])] = product(n, step[2], repeated[n])
-            elif n == IMAGES - 1 and step[2] == PASS_PAIRS[2][0]:
+                m = product(n, step[2], repeated[n])
+                if step[2] == 0:
+                    maps[(n, SAME)] = m
+                    if (n, FAR) not in maps:
+                        maps[(n, FAR)] = far_map()
+                    carry(maps[(n, FAR)], 0, 0, m, 1, 0, 32)
+                    carry(m, 1, 0, m, 0, 2, 33)
+                else:
+                    maps[(n, NEAR)] = m
+                    if (n, FAR) not in maps:
+                        maps[(n, FAR)] = far_map()
+                    carry(maps[(n, FAR)], 1, 0, m, 0, 2, 32)
+            elif n == IMAGES - 1 and step[2] == (6, 7):
                 for j in range(2):
                     for s in step[2]:
                         codes, scales = quantise(maps[(n, PASSES[s][0])], PASSES[s][1], j)

@@ -33,7 +33,7 @@ PASSES = (
     (SAME, 1, False),
 )
 LAST = len(PASSES) - 1
-IMAGE_GROUPS = ((0, 1), (1, IMAGES))
+IMAGE_GROUPS = ((0, 1), (1, 2), (2, IMAGES))
 RING = 14
 FIRST_W_STEP = 6
 W_AHEAD = 4
@@ -63,12 +63,14 @@ def tile_fast2order_de_conv_kernel(tc, x, W, out):
 
         w_rows = resident.tile([P, 2, 4096], BF16, name="w_rows")
         w_view = W.rearrange("(h o) f -> o h f", h=2)
-        for h in range(2):
-            for half in range(2):
-                nc.gpsimd.dma_start(
-                    out=w_rows[:, h, half * 2048 : (half + 1) * 2048],
-                    in_=w_view[:, h, half * 2048 : (half + 1) * 2048],
-                )
+
+        def load_w():
+            for h in range(2):
+                for half in range(2):
+                    nc.sync.dma_start(
+                        out=w_rows[:, h, half * 2048 : (half + 1) * 2048],
+                        in_=w_view[:, h, half * 2048 : (half + 1) * 2048],
+                    )
 
         ident_bf16 = resident.tile([P, P], BF16, name="ident_bf16")
         make_identity(nc, ident_bf16[:])
@@ -110,13 +112,18 @@ def tile_fast2order_de_conv_kernel(tc, x, W, out):
             )
 
         def image_rows(tiles, n, rows):
-            flat = tiles[0][:, 0, :] if n == 0 else tiles[1][:, n - 1, :]
+            g = min(n, len(IMAGE_GROUPS) - 1)
+            flat = tiles[g][:, n - IMAGE_GROUPS[g][0], :]
             return flat[:, 0 : rows * SIDE].rearrange("p (r z) -> p r z", z=SIDE)
 
-        for g in range(len(IMAGE_GROUPS)):
+        def load_x(g):
             load_first(g)
             load_second(1, g)
             load_second(0, g)
+
+        load_x(0)
+        load_w()
+        load_x(1)
 
         w_codes = resident.tile([P, 2048], U32, name="w_codes", align_bytes=64)
         w_scales = resident.tile([P, 2048], U8, name="w_scales", align_bytes=64)
@@ -190,8 +197,8 @@ def tile_fast2order_de_conv_kernel(tc, x, W, out):
             if m == SAME:
                 for v in range(2):
                     row = r + 2 * v
-                    src = w_pairs[:, :, row, :, row, :].rearrange("p g a u -> p u g a")
-                    nc.scalar.copy(out=by_v[:, :, :, :, v], in_=src)
+                    dst = by_v[:, :, :, :, v].rearrange("p u g a -> p g a u")
+                    nc.scalar.copy(out=dst, in_=w_pairs[:, :, row, :, row, :])
             else:
                 if m == NEAR:
                     row_a, row_t = r, slice(r + 1, r + 3)
@@ -200,10 +207,12 @@ def tile_fast2order_de_conv_kernel(tc, x, W, out):
                 if exchanged:
                     src = w_bf16[:, :, row_t, :, row_a, :]
                     src = src.rearrange("p g v t a -> p t g a v" if m == NEAR else "p g t v a -> p t g a v")
+                    nc.scalar.copy(out=by_v, in_=src)
                 else:
                     src = w_pairs[:, :, row_a, :, row_t, :]
-                    src = src.rearrange("p g a v u -> p u g a v" if m == NEAR else "p g v a u -> p u g a v")
-                nc.scalar.copy(out=by_v, in_=src)
+                    if m == FAR:
+                        src = src.rearrange("p g v a u -> p g a v u")
+                    nc.scalar.copy(out=by_v.rearrange("p u g a v -> p g a v u"), in_=src)
             sorted_w[s] = cols
 
         def transpose_w(s):
@@ -293,7 +302,7 @@ def tile_fast2order_de_conv_kernel(tc, x, W, out):
 
         for s in range(W_AHEAD):
             advance_w(s)
-            if s == 0:
+            if s == 1:
                 repeated[1] = repeat_first_factor(1)
 
         for index, step in enumerate(vector_steps()):
@@ -306,6 +315,8 @@ def tile_fast2order_de_conv_kernel(tc, x, W, out):
                         maps[(n, FAR)] = far_map()
                     carry(maps[(n, FAR)], 0, 0, m, 1, 0, 32)
                     carry(m, 1, 0, m, 0, 2, 33)
+                    if n == 0:
+                        load_x(2)
                 else:
                     maps[(n, NEAR)] = m
                     if (n, FAR) not in maps:
@@ -326,11 +337,12 @@ def tile_fast2order_de_conv_kernel(tc, x, W, out):
             s = index - FIRST_W_STEP
             if 0 <= s <= LAST:
                 quantise_w(s)
+                if s == LAST:
+                    repeated[3] = repeat_first_factor(3)
                 multiply_pass(0, s)
                 advance_w(s + W_AHEAD)
                 if s == 1:
                     repeated[2] = repeat_first_factor(2)
                 if s == LAST:
-                    repeated[3] = repeat_first_factor(3)
                     for s1 in range(LAST + 1):
                         multiply_pass(1, s1)

@@ -18,34 +18,53 @@ GRID = 32
 ROW = 4 * GRID
 X_PITCH = 1232
 
-SAME, NEAR, FAR = range(3)
+A, B, Y, Z = range(4)
 MAP_ROWS = 35
-DISTANCE = ((0, 3), (1, 2))
-PRODUCT_ROWS = (35, 34)
-PASSES = (
-    (NEAR, 0, False),
-    (NEAR, 0, True),
-    (NEAR, 1, False),
-    (NEAR, 1, True),
-    (FAR, 0, False),
-    (FAR, 0, True),
-    (SAME, 0, False),
-    (SAME, 1, False),
+PRODUCT_ROWS = (35, 33)
+FIRST_DISTANCE = (0, 2)
+CARRIED = (
+    (Z, 0, A, 1, 0, 33),
+    (Z, 1, A, 0, 2, 33),
+    (Y, 1, A, 1, 2, 32),
+    (Y, 0, B, 0, 1, 32),
 )
+PASSES = (
+    (A, 0, False),
+    (A, 1, False),
+    (B, 0, False),
+    (B, 0, True),
+    (Z, 0, True),
+    (Z, 1, True),
+    (Y, 0, False),
+    (Y, 0, True),
+)
+
+
+def window_rows(m, r):
+    return {
+        A: ((r, r), (r, r + 1)),
+        B: ((r, r + 2), (r, r + 3)),
+        Z: ((r, r + 1), (r + 2, r + 2)),
+        Y: ((r + 1, r + 3), (r + 2, r + 3)),
+    }[m]
+
+
 LAST = len(PASSES) - 1
 IMAGE_GROUPS = ((0, 1), (1, 2), (2, IMAGES))
 RING = 14
-FIRST_W_STEP = 6
+FIRST_W_STEP = 4
 W_AHEAD = 4
 
 
 def vector_steps():
-    steps = [("product", 0, 1), ("product", 0, 0)]
+    steps = [("product", 0, A), ("product", 0, B)]
     for n in range(IMAGES):
         steps += [("quantise", n, (0, 1)), ("quantise", n, (2, 3))]
-        if n + 1 < IMAGES:
-            steps += [("product", n + 1, 0), ("product", n + 1, 1)]
+        if 0 < n < IMAGES - 1:
+            steps += [("product", n + 1, A), ("product", n + 1, B)]
         steps += [("quantise", n, (4, 5)), ("quantise", n, (6, 7))]
+        if n == 0:
+            steps += [("product", 1, A), ("product", 1, B)]
     return steps
 
 
@@ -54,7 +73,8 @@ def tile_fast2order_de_conv_kernel(tc, x, W, out):
     with ExitStack() as ctx:
         resident = ctx.enter_context(tc.tile_pool(name="resident", bufs=1))
         repeated_pool = ctx.enter_context(tc.tile_pool(name="repeated", bufs=2))
-        map_pool = ctx.enter_context(tc.tile_pool(name="maps", bufs=2))
+        product_pool = ctx.enter_context(tc.tile_pool(name="products", bufs=1))
+        carried_pool = ctx.enter_context(tc.tile_pool(name="carried", bufs=2))
         ring = ctx.enter_context(tc.tile_pool(name="ring", bufs=RING))
         w_stage = ctx.enter_context(tc.tile_pool(name="w_stage", bufs=W_AHEAD))
         result_pool = ctx.enter_context(tc.tile_pool(name="results", bufs=4))
@@ -67,10 +87,12 @@ def tile_fast2order_de_conv_kernel(tc, x, W, out):
         def load_w():
             for h in range(2):
                 for half in range(2):
-                    nc.sync.dma_start(
+                    nc.gpsimd.dma_start(
                         out=w_rows[:, h, half * 2048 : (half + 1) * 2048],
                         in_=w_view[:, h, half * 2048 : (half + 1) * 2048],
                     )
+
+        load_w()
 
         ident_bf16 = resident.tile([P, P], BF16, name="ident_bf16")
         make_identity(nc, ident_bf16[:])
@@ -82,13 +104,14 @@ def tile_fast2order_de_conv_kernel(tc, x, W, out):
             resident.tile([P, n1 - n0, X_PITCH], BF16, name="first_%d" % n0) for (n0, n1) in IMAGE_GROUPS
         ]
         second = [
-            [resident.tile([P, n1 - n0, X_PITCH], BF16, name="second%d_%d" % (k, n0)) for (n0, n1) in IMAGE_GROUPS]
-            for k in range(2)
+            resident.tile([P, n1 - n0, X_PITCH], BF16, name="second_%d" % n0) for (n0, n1) in IMAGE_GROUPS
         ]
-        for g in range(len(IMAGE_GROUPS)):
-            for k in range(2):
-                unused = (SIDE - DISTANCE[k][1]) * SIDE // 16 * 16
-                nc.vector.memset(second[k][g][:, :, unused:X_PITCH], 0.0)
+        unused = (SIDE - 1) * SIDE // 16 * 16
+        for tile in second:
+            nc.vector.memset(tile[:, :, unused:X_PITCH], 0.0)
+
+        warm = resident.tile([P, 2], BF16, name="warm")
+        nc.scalar.copy(out=warm[:], in_=second[0][:, 0, X_PITCH - 2 : X_PITCH])
 
         def load_shifted(tiles, g, length, shift):
             n0, n1 = IMAGE_GROUPS[g]
@@ -103,33 +126,26 @@ def tile_fast2order_de_conv_kernel(tc, x, W, out):
         def load_first(g):
             load_shifted(first, g, lambda v: SIDE * SIDE - 3, lambda a, v: a)
 
-        def load_second(k, g):
-            load_shifted(
-                second[k],
-                g,
-                lambda v: min(PRODUCT_ROWS[k], SIDE - DISTANCE[k][v]) * SIDE,
-                lambda a, v: SIDE * DISTANCE[k][v],
-            )
+        def load_second(g):
+            load_shifted(second, g, lambda v: (SIDE - v) * SIDE, lambda a, v: v * SIDE)
 
-        def image_rows(tiles, n, rows):
+        def image_rows(tiles, n, row, rows):
             g = min(n, len(IMAGE_GROUPS) - 1)
             flat = tiles[g][:, n - IMAGE_GROUPS[g][0], :]
-            return flat[:, 0 : rows * SIDE].rearrange("p (r z) -> p r z", z=SIDE)
+            return flat[:, row * SIDE : (row + rows) * SIDE].rearrange("p (r z) -> p r z", z=SIDE)
 
         def load_x(g):
             load_first(g)
-            load_second(1, g)
-            load_second(0, g)
+            load_second(g)
 
         load_x(0)
-        load_w()
         load_x(1)
 
         w_codes = resident.tile([P, 2048], U32, name="w_codes", align_bytes=64)
         w_scales = resident.tile([P, 2048], U8, name="w_scales", align_bytes=64)
 
         def repeat_first_factor(n):
-            columns = image_rows(first, n, MAP_ROWS)[:, :, 0:GRID].rearrange("p r (w q) -> p r w q", q=4)
+            columns = image_rows(first, n, 0, MAP_ROWS)[:, :, 0:GRID].rearrange("p r (w q) -> p r w q", q=4)
             tiles = []
             for q in range(4):
                 rep = repeated_pool.tile([P, MAP_ROWS, 8, 4], BF16, name="rep%d" % q)
@@ -143,12 +159,9 @@ def tile_fast2order_de_conv_kernel(tc, x, W, out):
 
         def product(n, k, rep):
             rows = PRODUCT_ROWS[k]
-            if k == 0:
-                m = map_pool.tile([P, MAP_ROWS * ROW], BF16, name="same", align_bytes=64)
-            else:
-                m = map_pool.tile([P, MAP_ROWS * ROW], BF16, name="near", align_bytes=64, bufs=1)
+            m = product_pool.tile([P, MAP_ROWS * ROW], BF16, name="map%d" % k, align_bytes=64)
             by_q = m[:].rearrange("p (r q e) -> p r q e", q=4, e=GRID)
-            factor = image_rows(second[k], n, rows)
+            factor = image_rows(second, n, FIRST_DISTANCE[k], rows)
             for q in range(4):
                 nc.vector.tensor_tensor(
                     out=by_q[:, 0:rows, q, :],
@@ -158,14 +171,16 @@ def tile_fast2order_de_conv_kernel(tc, x, W, out):
                 )
             return m
 
-        def carry(to, to_v, to_row, source, from_v, from_row, rows):
-            nc.sync.dma_start(
-                out=to[to_v:P:2, to_row * ROW : (to_row + rows) * ROW],
-                in_=source[from_v:P:2, from_row * ROW : (from_row + rows) * ROW],
-            )
-
-        def far_map():
-            return map_pool.tile([P, MAP_ROWS * ROW], BF16, name="far", align_bytes=64)
+        def carry(n, k):
+            for to, to_v, source, from_v, row, rows in CARRIED:
+                if source != k:
+                    continue
+                if (n, to) not in maps:
+                    maps[(n, to)] = carried_pool.tile([P, 33 * ROW], BF16, name="map%d" % to, align_bytes=64)
+                nc.sync.dma_start(
+                    out=maps[(n, to)][to_v:P:2, 0 : rows * ROW],
+                    in_=maps[(n, source)][from_v:P:2, row * ROW : (row + rows) * ROW],
+                )
 
         def quantise(m, r, j=None):
             cols = 1024 if j is None else 512
@@ -194,23 +209,26 @@ def tile_fast2order_de_conv_kernel(tc, x, W, out):
             else:
                 cols = w_stage.tile([P, 2, 2, P], F32, name="w_col_pairs")
             by_v = cols[:].rearrange("p t h (c a v) -> p t (h c) a v", a=4, v=2)
-            if m == SAME:
-                for v in range(2):
-                    row = r + 2 * v
-                    dst = by_v[:, :, :, :, v].rearrange("p u g a -> p g a u")
-                    nc.scalar.copy(out=dst, in_=w_pairs[:, :, row, :, row, :])
+            (a0, t0), (a1, t1) = window_rows(m, r)
+            if a0 != a1 and t0 != t1:
+                for v, (row_a, row_t) in enumerate(window_rows(m, r)):
+                    dst = by_v[:, :, :, :, v]
+                    if exchanged:
+                        src = w_bf16[:, :, row_t, :, row_a, :].rearrange("p g t a -> p t g a")
+                    else:
+                        src = w_pairs[:, :, row_a, :, row_t, :]
+                        dst = dst.rearrange("p u g a -> p g a u")
+                    nc.scalar.copy(out=dst, in_=src)
             else:
-                if m == NEAR:
-                    row_a, row_t = r, slice(r + 1, r + 3)
-                else:
-                    row_a, row_t = slice(0, 3, 2), 3
+                row_a = a0 if a0 == a1 else slice(a0, a1 + 1)
+                row_t = t0 if t0 == t1 else slice(t0, t1 + 1)
                 if exchanged:
                     src = w_bf16[:, :, row_t, :, row_a, :]
-                    src = src.rearrange("p g v t a -> p t g a v" if m == NEAR else "p g t v a -> p t g a v")
+                    src = src.rearrange("p g t v a -> p t g a v" if t0 == t1 else "p g v t a -> p t g a v")
                     nc.scalar.copy(out=by_v, in_=src)
                 else:
                     src = w_pairs[:, :, row_a, :, row_t, :]
-                    if m == FAR:
+                    if a0 != a1:
                         src = src.rearrange("p g v a u -> p g a v u")
                     nc.scalar.copy(out=by_v.rearrange("p u g a v -> p g a v u"), in_=src)
             sorted_w[s] = cols
@@ -300,28 +318,11 @@ def tile_fast2order_de_conv_kernel(tc, x, W, out):
                 for j in range(2):
                     store(n, sums_of[n], j)
 
-        for s in range(W_AHEAD):
-            advance_w(s)
-            if s == 1:
-                repeated[1] = repeat_first_factor(1)
-
         for index, step in enumerate(vector_steps()):
             n = step[1]
             if step[0] == "product":
-                m = product(n, step[2], repeated[n])
-                if step[2] == 0:
-                    maps[(n, SAME)] = m
-                    if (n, FAR) not in maps:
-                        maps[(n, FAR)] = far_map()
-                    carry(maps[(n, FAR)], 0, 0, m, 1, 0, 32)
-                    carry(m, 1, 0, m, 0, 2, 33)
-                    if n == 0:
-                        load_x(2)
-                else:
-                    maps[(n, NEAR)] = m
-                    if (n, FAR) not in maps:
-                        maps[(n, FAR)] = far_map()
-                    carry(maps[(n, FAR)], 1, 0, m, 0, 2, 32)
+                maps[(n, step[2])] = product(n, step[2], repeated[n])
+                carry(n, step[2])
             elif n == IMAGES - 1 and step[2] == (6, 7):
                 for j in range(2):
                     for s in step[2]:
@@ -331,18 +332,25 @@ def tile_fast2order_de_conv_kernel(tc, x, W, out):
             else:
                 for s in step[2]:
                     quantised[(n, s)] = quantise(maps[(n, PASSES[s][0])], PASSES[s][1])
-                if n >= 2:
+                if index > FIRST_W_STEP + LAST:
                     for s in step[2]:
                         multiply_pass(n, s)
             s = index - FIRST_W_STEP
+            if index == 1:
+                load_x(2)
+                for s0 in range(W_AHEAD):
+                    advance_w(s0)
+                    if s0 == 2:
+                        repeated[1] = repeat_first_factor(1)
             if 0 <= s <= LAST:
                 quantise_w(s)
                 if s == LAST:
                     repeated[3] = repeat_first_factor(3)
                 multiply_pass(0, s)
                 advance_w(s + W_AHEAD)
-                if s == 1:
+                if s == 0:
                     repeated[2] = repeat_first_factor(2)
                 if s == LAST:
                     for s1 in range(LAST + 1):
-                        multiply_pass(1, s1)
+                        if (1, s1) in quantised:
+                            multiply_pass(1, s1)

@@ -51,8 +51,10 @@ def window_rows(m, r):
 
 LAST = len(PASSES) - 1
 IMAGE_GROUPS = ((0, 1), (1, 2), (2, IMAGES))
+COLUMN_GROUPS = (((0, 512), (512, 512)),) * (IMAGES - 1) + (((0, 512), (512, 256), (768, 256)),)
 RING = 14
-FIRST_W_STEP = 4
+FIRST_W_STEP = 5
+LAST_W_STEP = FIRST_W_STEP + LAST - 1
 W_AHEAD = 4
 
 
@@ -145,28 +147,28 @@ def tile_fast2order_de_conv_kernel(tc, x, W, out):
         w_scales = resident.tile([P, 2048], U8, name="w_scales", align_bytes=64)
 
         def repeat_first_factor(n):
-            columns = image_rows(first, n, 0, MAP_ROWS)[:, :, 0:GRID].rearrange("p r (w q) -> p r w q", q=4)
-            tiles = []
-            for q in range(4):
-                rep = repeated_pool.tile([P, MAP_ROWS, 8, 4], BF16, name="rep%d" % q)
-                one = columns[:, :, :, q : q + 1].to_broadcast([P, MAP_ROWS, 8, 4])
-                if n == 0 and q < 2:
-                    nc.vector.tensor_copy(out=rep[:], in_=one)
-                else:
-                    nc.scalar.copy(out=rep[:], in_=one)
-                tiles.append(rep)
-            return tiles
+            pairs = repeated_pool.tile([P, MAP_ROWS, GRID, 2], BF16, name="pairs")
+            columns = image_rows(first, n, 0, MAP_ROWS)[:, :, 0:GRID].unsqueeze(3)
+            if n > 0:
+                nc.scalar.copy(out=pairs[:], in_=columns.to_broadcast([P, MAP_ROWS, GRID, 2]))
+                return pairs
+            half = MAP_ROWS // 2 + 1
+            nc.vector.tensor_copy(out=pairs[:, 0:half], in_=columns[:, 0:half].to_broadcast([P, half, GRID, 2]))
+            rest = MAP_ROWS - half
+            nc.scalar.copy(out=pairs[:, half:], in_=columns[:, half:].to_broadcast([P, rest, GRID, 2]))
+            return pairs
 
-        def product(n, k, rep):
+        def product(n, k, pairs):
             rows = PRODUCT_ROWS[k]
             m = product_pool.tile([P, MAP_ROWS * ROW], BF16, name="map%d" % k, align_bytes=64)
             by_q = m[:].rearrange("p (r q e) -> p r q e", q=4, e=GRID)
             factor = image_rows(second, n, FIRST_DISTANCE[k], rows)
+            one = pairs[:, 0:rows].rearrange("p r (w q) u -> p r w q u", q=4)
             for q in range(4):
                 nc.vector.tensor_tensor(
-                    out=by_q[:, 0:rows, q, :],
-                    in0=rep[q][:, 0:rows].rearrange("p r w t -> p r (w t)"),
-                    in1=factor[:, :, q : q + GRID],
+                    out=by_q[:, 0:rows, q, :].rearrange("p r (w t u) -> p r w t u", t=2, u=2),
+                    in0=one[:, :, :, q : q + 1, :].to_broadcast([P, rows, 8, 2, 2]),
+                    in1=factor[:, :, q : q + GRID].rearrange("p r (w t u) -> p r w t u", t=2, u=2),
                     op=mybir.AluOpType.mult,
                 )
             return m
@@ -182,17 +184,15 @@ def tile_fast2order_de_conv_kernel(tc, x, W, out):
                     in_=maps[(n, source)][from_v:P:2, row * ROW : (row + rows) * ROW],
                 )
 
-        def quantise(m, r, j=None):
-            cols = 1024 if j is None else 512
-            start = r * ROW + (0 if j is None else j * 4 * cols)
-            kind = "" if j is None else "_half"
-            depth = RING if j is None else 4
-            codes = ring.tile([P, cols], U32, name="codes" + kind, align_bytes=64, bufs=depth)
-            scales = ring.tile([P, cols], U8, name="scales" + kind, align_bytes=64, bufs=depth)
+        def quantise(m, r, start=0, columns=1024):
+            at = r * ROW + 4 * start
+            depth = RING if columns == 1024 else 4
+            codes = ring.tile([P, columns], U32, name="codes%d" % columns, align_bytes=64, bufs=depth)
+            scales = ring.tile([P, columns], U8, name="scales%d" % columns, align_bytes=64, bufs=depth)
             nc.vector.quantize_mx(
                 out=codes[:].bitcast(FP8X4),
                 scales=scales[:],
-                in_=m[:, start : start + 4 * cols],
+                in_=m[:, at : at + 4 * columns],
             )
             return codes, scales
 
@@ -247,13 +247,14 @@ def tile_fast2order_de_conv_kernel(tc, x, W, out):
             transposed_w[s] = bank
 
         def group_w(s):
-            grouped = w_stage.tile([P, 1024], BF16, name="w_grouped", align_bytes=64)
+            if s % 2 == 0:
+                grouped_w[s // 2] = w_stage.tile([P, 2048], BF16, name="w_grouped", align_bytes=64, bufs=3)
+            grouped = grouped_w[s // 2][:, s % 2 * 1024 : (s % 2 + 1) * 1024]
             if PASSES[s][2]:
-                dst = grouped[:].rearrange("p (h o t) -> p h o t", h=2, t=4)
+                dst = grouped.rearrange("p (h o t) -> p h o t", h=2, t=4)
             else:
-                dst = grouped[:].bitcast(F32).rearrange("p (h o t) -> p h o t", h=2, t=2)
+                dst = grouped.bitcast(F32).rearrange("p (h o t) -> p h o t", h=2, t=2)
             nc.scalar.copy(out=dst, in_=transposed_w[s][:].rearrange("p t h o -> p h o t"))
-            grouped_w[s] = grouped
 
         def advance_w(s):
             if s <= LAST:
@@ -262,46 +263,47 @@ def tile_fast2order_de_conv_kernel(tc, x, W, out):
             if 1 <= s <= LAST + 1:
                 group_w(s - 1)
 
-        def quantise_w(s):
+        def quantise_w(k):
             nc.vector.quantize_mx(
-                out=w_codes[:, s * 256 : (s + 1) * 256].bitcast(FP8X4),
-                scales=w_scales[:, s * 256 : (s + 1) * 256],
-                in_=grouped_w[s][:],
+                out=w_codes[:, k * 512 : (k + 1) * 512].bitcast(FP8X4),
+                scales=w_scales[:, k * 512 : (k + 1) * 512],
+                in_=grouped_w[k][:],
             )
 
-        def multiply(s, sums, codes, scales, j, at):
+        def multiply(n, s, g, codes, scales, at):
+            columns = COLUMN_GROUPS[n][g][1]
             for h in range(2):
                 lo = s * 256 + h * P
                 nc.tensor.matmul_mx(
-                    out=sums[(j, h)][:],
+                    out=sums_of[n][(g, h)][:, 0:columns],
                     lhsT=w_codes[:, lo : lo + P].bitcast(FP8X4),
                     lhsT_scale=w_scales[:, lo : lo + P],
-                    rhs=codes[:, at : at + 512].bitcast(FP8X4),
-                    rhs_scale=scales[:, at : at + 512],
+                    rhs=codes[:, at : at + columns].bitcast(FP8X4),
+                    rhs_scale=scales[:, at : at + columns],
                     start=(s == 0),
                     stop=(s == LAST),
                 )
 
-        def new_sums():
+        def new_sums(n):
             sums = {}
-            for j in range(2):
+            for g in range(len(COLUMN_GROUPS[n])):
                 for h in range(2):
-                    sums[(j, h)] = banks.tile([P, 512], F32, name="sums", tag="bank")
+                    sums[(g, h)] = banks.tile([P, 512], F32, name="sums", tag="bank")
             return sums
 
-        def store(n, sums, j):
+        def store(n, g):
+            start, columns = COLUMN_GROUPS[n][g]
             for h in range(2):
-                res = result_pool.tile([P, 512], F32, name="res")
+                res = result_pool.tile([P, columns], F32, name="res%d" % columns)
                 dst = res[:].rearrange("p (y w q) -> p y w q", w=8, q=4)
-                src = sums[(j, h)][:].rearrange("p (y q w) -> p y w q", q=4, w=8)
-                if n == IMAGES - 1 and j == 1 and h == 1:
+                src = sums_of[n][(g, h)][:, 0:columns].rearrange("p (y q w) -> p y w q", q=4, w=8)
+                rows = out[n, h * P : (h + 1) * P, start // GRID : (start + columns) // GRID, :]
+                if n == IMAGES - 1 and g == len(COLUMN_GROUPS[n]) - 1 and h == 1:
                     nc.vector.tensor_copy(out=dst, in_=src)
                 else:
                     nc.scalar.copy(out=dst, in_=src)
-                nc.scalar.dma_start(
-                    out=out[n, h * P : (h + 1) * P, j * 16 : (j + 1) * 16, :].rearrange("o y z -> o (y z)"),
-                    in_=res[:],
-                )
+                queue = nc.sync if n == IMAGES - 1 else nc.scalar
+                queue.dma_start(out=rows.rearrange("o y z -> o (y z)"), in_=res[:])
 
         repeated = {0: repeat_first_factor(0)}
         maps = {}
@@ -310,13 +312,13 @@ def tile_fast2order_de_conv_kernel(tc, x, W, out):
 
         def multiply_pass(n, s):
             if s == 0:
-                sums_of[n] = new_sums()
+                sums_of[n] = new_sums(n)
             codes, scales = quantised[(n, s)]
-            for j in range(2):
-                multiply(s, sums_of[n], codes, scales, j, j * 512)
+            for g in range(len(COLUMN_GROUPS[n])):
+                multiply(n, s, g, codes, scales, COLUMN_GROUPS[n][g][0])
             if s == LAST:
-                for j in range(2):
-                    store(n, sums_of[n], j)
+                for g in range(len(COLUMN_GROUPS[n])):
+                    store(n, g)
 
         for index, step in enumerate(vector_steps()):
             n = step[1]
@@ -324,33 +326,33 @@ def tile_fast2order_de_conv_kernel(tc, x, W, out):
                 maps[(n, step[2])] = product(n, step[2], repeated[n])
                 carry(n, step[2])
             elif n == IMAGES - 1 and step[2] == (6, 7):
-                for j in range(2):
+                for g, (start, columns) in enumerate(COLUMN_GROUPS[n]):
                     for s in step[2]:
-                        codes, scales = quantise(maps[(n, PASSES[s][0])], PASSES[s][1], j)
-                        multiply(s, sums_of[n], codes, scales, j, 0)
-                    store(n, sums_of[n], j)
+                        codes, scales = quantise(maps[(n, PASSES[s][0])], PASSES[s][1], start, columns)
+                        multiply(n, s, g, codes, scales, 0)
+                    store(n, g)
             else:
                 for s in step[2]:
                     quantised[(n, s)] = quantise(maps[(n, PASSES[s][0])], PASSES[s][1])
-                if index > FIRST_W_STEP + LAST:
+                if index > LAST_W_STEP:
                     for s in step[2]:
                         multiply_pass(n, s)
-            s = index - FIRST_W_STEP
             if index == 1:
                 load_x(2)
-                for s0 in range(W_AHEAD):
-                    advance_w(s0)
-                    if s0 == 2:
+                for s in range(W_AHEAD):
+                    advance_w(s)
+                    if s == 2:
                         repeated[1] = repeat_first_factor(1)
-            if 0 <= s <= LAST:
-                quantise_w(s)
-                if s == LAST:
+            if FIRST_W_STEP <= index <= LAST_W_STEP and (index - FIRST_W_STEP) % 2 == 0:
+                quantise_w((index - FIRST_W_STEP) // 2)
+                if index == LAST_W_STEP:
                     repeated[3] = repeat_first_factor(3)
-                multiply_pass(0, s)
-                advance_w(s + W_AHEAD)
-                if s == 0:
-                    repeated[2] = repeat_first_factor(2)
-                if s == LAST:
-                    for s1 in range(LAST + 1):
-                        if (1, s1) in quantised:
-                            multiply_pass(1, s1)
+                for s in (index - FIRST_W_STEP, index - FIRST_W_STEP + 1):
+                    multiply_pass(0, s)
+                    advance_w(s + W_AHEAD)
+                    if s == 0:
+                        repeated[2] = repeat_first_factor(2)
+                if index == LAST_W_STEP:
+                    for s in range(LAST + 1):
+                        if (1, s) in quantised:
+                            multiply_pass(1, s)

@@ -147,28 +147,28 @@ def tile_fast2order_de_conv_kernel(tc, x, W, out):
         w_scales = resident.tile([P, 2048], U8, name="w_scales", align_bytes=64)
 
         def repeat_first_factor(n):
-            pairs = repeated_pool.tile([P, MAP_ROWS, GRID, 2], BF16, name="pairs")
-            columns = image_rows(first, n, 0, MAP_ROWS)[:, :, 0:GRID].unsqueeze(3)
-            if n > 0:
-                nc.scalar.copy(out=pairs[:], in_=columns.to_broadcast([P, MAP_ROWS, GRID, 2]))
-                return pairs
-            half = MAP_ROWS // 2 + 1
-            nc.vector.tensor_copy(out=pairs[:, 0:half], in_=columns[:, 0:half].to_broadcast([P, half, GRID, 2]))
-            rest = MAP_ROWS - half
-            nc.scalar.copy(out=pairs[:, half:], in_=columns[:, half:].to_broadcast([P, rest, GRID, 2]))
-            return pairs
+            columns = image_rows(first, n, 0, MAP_ROWS)[:, :, 0:GRID].rearrange("p r (w q) -> p r w q", q=4)
+            tiles = []
+            for q in range(4):
+                rep = repeated_pool.tile([P, MAP_ROWS, 8, 4], BF16, name="rep%d" % q)
+                one = columns[:, :, :, q : q + 1].to_broadcast([P, MAP_ROWS, 8, 4])
+                if n == 0 and q < 2:
+                    nc.vector.tensor_copy(out=rep[:], in_=one)
+                else:
+                    nc.scalar.copy(out=rep[:], in_=one)
+                tiles.append(rep)
+            return tiles
 
-        def product(n, k, pairs):
+        def product(n, k, rep):
             rows = PRODUCT_ROWS[k]
             m = product_pool.tile([P, MAP_ROWS * ROW], BF16, name="map%d" % k, align_bytes=64)
             by_q = m[:].rearrange("p (r q e) -> p r q e", q=4, e=GRID)
             factor = image_rows(second, n, FIRST_DISTANCE[k], rows)
-            one = pairs[:, 0:rows].rearrange("p r (w q) u -> p r w q u", q=4)
             for q in range(4):
                 nc.vector.tensor_tensor(
-                    out=by_q[:, 0:rows, q, :].rearrange("p r (w t u) -> p r w t u", t=2, u=2),
-                    in0=one[:, :, :, q : q + 1, :].to_broadcast([P, rows, 8, 2, 2]),
-                    in1=factor[:, :, q : q + GRID].rearrange("p r (w t u) -> p r w t u", t=2, u=2),
+                    out=by_q[:, 0:rows, q, :],
+                    in0=rep[q][:, 0:rows].rearrange("p r w t -> p r (w t)"),
+                    in1=factor[:, :, q : q + GRID],
                     op=mybir.AluOpType.mult,
                 )
             return m

@@ -17,6 +17,7 @@ SIDE = 35
 GRID = 32
 ROW = 4 * GRID
 X_PITCH = 1232
+ALIGNED_PITCH = 40
 
 A, B, Y, Z = range(4)
 MAP_ROWS = 35
@@ -52,9 +53,9 @@ def window_rows(m, r):
 LAST = len(PASSES) - 1
 IMAGE_GROUPS = ((0, 1), (1, 2), (2, IMAGES))
 COLUMN_GROUPS = (((0, 512), (512, 512)),) * (IMAGES - 1) + (((0, 512), (512, 256), (768, 256)),)
-RING = 14
-FIRST_W_STEP = 5
-LAST_W_STEP = FIRST_W_STEP + LAST - 1
+RING = 12
+FIRST_W_STEP = 4
+LAST_W_STEP = FIRST_W_STEP + LAST
 W_AHEAD = 4
 
 
@@ -77,8 +78,9 @@ def tile_fast2order_de_conv_kernel(tc, x, W, out):
         repeated_pool = ctx.enter_context(tc.tile_pool(name="repeated", bufs=2))
         product_pool = ctx.enter_context(tc.tile_pool(name="products", bufs=1))
         carried_pool = ctx.enter_context(tc.tile_pool(name="carried", bufs=2))
+        aligned_pool = ctx.enter_context(tc.tile_pool(name="aligned", bufs=2))
         ring = ctx.enter_context(tc.tile_pool(name="ring", bufs=RING))
-        w_stage = ctx.enter_context(tc.tile_pool(name="w_stage", bufs=W_AHEAD))
+        w_stage = ctx.enter_context(tc.tile_pool(name="w_stage", bufs=3))
         result_pool = ctx.enter_context(tc.tile_pool(name="results", bufs=4))
         banks = ctx.enter_context(tc.psum_pool(name="banks", bufs=8))
         ctx.enter_context(tc.manual_schedule())
@@ -147,28 +149,39 @@ def tile_fast2order_de_conv_kernel(tc, x, W, out):
         w_scales = resident.tile([P, 2048], U8, name="w_scales", align_bytes=64)
 
         def repeat_first_factor(n):
-            columns = image_rows(first, n, 0, MAP_ROWS)[:, :, 0:GRID].rearrange("p r (w q) -> p r w q", q=4)
+            pairs = repeated_pool.tile([P, 4, MAP_ROWS, 8, 2], BF16, name="pairs")
+            columns = image_rows(first, n, 0, MAP_ROWS)[:, :, 0:GRID].rearrange("p r (w q) -> p q r w", q=4).unsqueeze(4)
+            if n == 0:
+                nc.vector.tensor_copy(out=pairs[:, 0:2], in_=columns[:, 0:2].to_broadcast([P, 2, MAP_ROWS, 8, 2]))
+                nc.scalar.copy(out=pairs[:, 2:4], in_=columns[:, 2:4].to_broadcast([P, 2, MAP_ROWS, 8, 2]))
+            else:
+                nc.scalar.copy(out=pairs[:], in_=columns.to_broadcast([P, 4, MAP_ROWS, 8, 2]))
+            return pairs
+
+        def align_second_factor(n):
+            rows = image_rows(second, n, 0, MAP_ROWS)
             tiles = []
-            for q in range(4):
-                rep = repeated_pool.tile([P, MAP_ROWS, 8, 4], BF16, name="rep%d" % q)
-                one = columns[:, :, :, q : q + 1].to_broadcast([P, MAP_ROWS, 8, 4])
-                if n == 0 and q < 2:
-                    nc.vector.tensor_copy(out=rep[:], in_=one)
-                else:
-                    nc.scalar.copy(out=rep[:], in_=one)
-                tiles.append(rep)
+            for odd in range(2):
+                aligned = aligned_pool.tile([P, MAP_ROWS, ALIGNED_PITCH], BF16, name="aligned%d" % odd)
+                nc.scalar.copy(out=aligned[:, :, 0:34], in_=rows[:, :, odd : odd + 34])
+                tiles.append(aligned)
             return tiles
 
-        def product(n, k, rep):
+        def product(n, k, pairs):
             rows = PRODUCT_ROWS[k]
             m = product_pool.tile([P, MAP_ROWS * ROW], BF16, name="map%d" % k, align_bytes=64)
             by_q = m[:].rearrange("p (r q e) -> p r q e", q=4, e=GRID)
-            factor = image_rows(second, n, FIRST_DISTANCE[k], rows)
+            if n in aligned_second:
+                low = FIRST_DISTANCE[k]
+                factors = [aligned_second[n][q % 2][:, low : low + rows, q - q % 2 : q - q % 2 + GRID] for q in range(4)]
+            else:
+                factor = image_rows(second, n, FIRST_DISTANCE[k], rows)
+                factors = [factor[:, :, q : q + GRID] for q in range(4)]
             for q in range(4):
                 nc.vector.tensor_tensor(
-                    out=by_q[:, 0:rows, q, :],
-                    in0=rep[q][:, 0:rows].rearrange("p r w t -> p r (w t)"),
-                    in1=factor[:, :, q : q + GRID],
+                    out=by_q[:, 0:rows, q, :].rearrange("p r (w t u) -> p r w t u", t=2, u=2),
+                    in0=pairs[:, q, 0:rows].unsqueeze(3).to_broadcast([P, rows, 8, 2, 2]),
+                    in1=factors[q].rearrange("p r (w t u) -> p r w t u", t=2, u=2),
                     op=mybir.AluOpType.mult,
                 )
             return m
@@ -247,14 +260,13 @@ def tile_fast2order_de_conv_kernel(tc, x, W, out):
             transposed_w[s] = bank
 
         def group_w(s):
-            if s % 2 == 0:
-                grouped_w[s // 2] = w_stage.tile([P, 2048], BF16, name="w_grouped", align_bytes=64, bufs=3)
-            grouped = grouped_w[s // 2][:, s % 2 * 1024 : (s % 2 + 1) * 1024]
+            grouped = w_stage.tile([P, 1024], BF16, name="w_grouped", align_bytes=64, bufs=4)
             if PASSES[s][2]:
-                dst = grouped.rearrange("p (h o t) -> p h o t", h=2, t=4)
+                dst = grouped[:].rearrange("p (h o t) -> p h o t", h=2, t=4)
             else:
-                dst = grouped.bitcast(F32).rearrange("p (h o t) -> p h o t", h=2, t=2)
+                dst = grouped[:].bitcast(F32).rearrange("p (h o t) -> p h o t", h=2, t=2)
             nc.scalar.copy(out=dst, in_=transposed_w[s][:].rearrange("p t h o -> p h o t"))
+            grouped_w[s] = grouped
 
         def advance_w(s):
             if s <= LAST:
@@ -263,19 +275,21 @@ def tile_fast2order_de_conv_kernel(tc, x, W, out):
             if 1 <= s <= LAST + 1:
                 group_w(s - 1)
 
-        def quantise_w(k):
+        def quantise_w(s):
             nc.vector.quantize_mx(
-                out=w_codes[:, k * 512 : (k + 1) * 512].bitcast(FP8X4),
-                scales=w_scales[:, k * 512 : (k + 1) * 512],
-                in_=grouped_w[k][:],
+                out=w_codes[:, s * 256 : (s + 1) * 256].bitcast(FP8X4),
+                scales=w_scales[:, s * 256 : (s + 1) * 256],
+                in_=grouped_w[s][:],
             )
 
         def multiply(n, s, g, codes, scales, at):
             columns = COLUMN_GROUPS[n][g][1]
             for h in range(2):
+                if s == 0:
+                    sums_of[(n, g, h)] = banks.tile([P, 512], F32, name="sums", tag="bank")
                 lo = s * 256 + h * P
                 nc.tensor.matmul_mx(
-                    out=sums_of[n][(g, h)][:, 0:columns],
+                    out=sums_of[(n, g, h)][:, 0:columns],
                     lhsT=w_codes[:, lo : lo + P].bitcast(FP8X4),
                     lhsT_scale=w_scales[:, lo : lo + P],
                     rhs=codes[:, at : at + columns].bitcast(FP8X4),
@@ -284,19 +298,12 @@ def tile_fast2order_de_conv_kernel(tc, x, W, out):
                     stop=(s == LAST),
                 )
 
-        def new_sums(n):
-            sums = {}
-            for g in range(len(COLUMN_GROUPS[n])):
-                for h in range(2):
-                    sums[(g, h)] = banks.tile([P, 512], F32, name="sums", tag="bank")
-            return sums
-
         def store(n, g):
             start, columns = COLUMN_GROUPS[n][g]
             for h in range(2):
                 res = result_pool.tile([P, columns], F32, name="res%d" % columns)
                 dst = res[:].rearrange("p (y w q) -> p y w q", w=8, q=4)
-                src = sums_of[n][(g, h)][:, 0:columns].rearrange("p (y q w) -> p y w q", q=4, w=8)
+                src = sums_of[(n, g, h)][:, 0:columns].rearrange("p (y q w) -> p y w q", q=4, w=8)
                 rows = out[n, h * P : (h + 1) * P, start // GRID : (start + columns) // GRID, :]
                 if n == IMAGES - 1 and g == len(COLUMN_GROUPS[n]) - 1 and h == 1:
                     nc.vector.tensor_copy(out=dst, in_=src)
@@ -306,19 +313,22 @@ def tile_fast2order_de_conv_kernel(tc, x, W, out):
                 queue.dma_start(out=rows.rearrange("o y z -> o (y z)"), in_=res[:])
 
         repeated = {0: repeat_first_factor(0)}
+        aligned_second = {}
         maps = {}
         sums_of = {}
         quantised = {}
 
-        def multiply_pass(n, s):
-            if s == 0:
-                sums_of[n] = new_sums(n)
+        def multiply_pass(n, s, groups):
             codes, scales = quantised[(n, s)]
-            for g in range(len(COLUMN_GROUPS[n])):
+            for g in groups:
                 multiply(n, s, g, codes, scales, COLUMN_GROUPS[n][g][0])
-            if s == LAST:
-                for g in range(len(COLUMN_GROUPS[n])):
+                if s == LAST:
                     store(n, g)
+
+        def multiply_all(n, s):
+            multiply_pass(n, s, range(len(COLUMN_GROUPS[n])))
+
+        early = []
 
         for index, step in enumerate(vector_steps()):
             n = step[1]
@@ -336,23 +346,29 @@ def tile_fast2order_de_conv_kernel(tc, x, W, out):
                     quantised[(n, s)] = quantise(maps[(n, PASSES[s][0])], PASSES[s][1])
                 if index > LAST_W_STEP:
                     for s in step[2]:
-                        multiply_pass(n, s)
+                        multiply_all(n, s)
             if index == 1:
                 load_x(2)
                 for s in range(W_AHEAD):
                     advance_w(s)
-                    if s == 2:
+                    if s == 1:
                         repeated[1] = repeat_first_factor(1)
-            if FIRST_W_STEP <= index <= LAST_W_STEP and (index - FIRST_W_STEP) % 2 == 0:
-                quantise_w((index - FIRST_W_STEP) // 2)
-                if index == LAST_W_STEP:
+                        aligned_second[1] = align_second_factor(1)
+            s = index - FIRST_W_STEP
+            if 0 <= s <= LAST:
+                quantise_w(s)
+                if s == LAST:
                     repeated[3] = repeat_first_factor(3)
-                for s in (index - FIRST_W_STEP, index - FIRST_W_STEP + 1):
-                    multiply_pass(0, s)
-                    advance_w(s + W_AHEAD)
-                    if s == 0:
-                        repeated[2] = repeat_first_factor(2)
-                if index == LAST_W_STEP:
-                    for s in range(LAST + 1):
-                        if (1, s) in quantised:
-                            multiply_pass(1, s)
+                    aligned_second[3] = align_second_factor(3)
+                multiply_all(0, s)
+                while len(early) < LAST and len(early) <= s and (1, len(early)) in quantised:
+                    multiply_pass(1, len(early), (0,))
+                    early.append(len(early))
+                advance_w(s + W_AHEAD)
+                if s == 0:
+                    repeated[2] = repeat_first_factor(2)
+                    aligned_second[2] = align_second_factor(2)
+                if s == LAST:
+                    for s1 in range(LAST + 1):
+                        if (1, s1) in quantised:
+                            multiply_pass(1, s1, (1,) if s1 in early else (0, 1))

@@ -54,7 +54,7 @@ LAST = len(PASSES) - 1
 IMAGE_GROUPS = ((0, 1), (1, 2), (2, IMAGES))
 COLUMN_GROUPS = (((0, 512), (512, 512)),) * (IMAGES - 1) + (((0, 512), (512, 256), (768, 256)),)
 RING = 12
-FIRST_W_STEP = 4
+FIRST_W_STEP = 3
 LAST_W_STEP = FIRST_W_STEP + LAST
 W_AHEAD = 4
 
@@ -163,7 +163,8 @@ def tile_fast2order_de_conv_kernel(tc, x, W, out):
             tiles = []
             for odd in range(2):
                 aligned = aligned_pool.tile([P, MAP_ROWS, ALIGNED_PITCH], BF16, name="aligned%d" % odd)
-                nc.scalar.copy(out=aligned[:, :, 0:34], in_=rows[:, :, odd : odd + 34])
+                copy = nc.vector.tensor_copy if n < 2 else nc.scalar.copy
+                copy(out=aligned[:, :, 0:34], in_=rows[:, :, odd : odd + 34])
                 tiles.append(aligned)
             return tiles
 
@@ -333,6 +334,8 @@ def tile_fast2order_de_conv_kernel(tc, x, W, out):
         for index, step in enumerate(vector_steps()):
             n = step[1]
             if step[0] == "product":
+                if step[2] == A and n < 2:
+                    aligned_second[n] = align_second_factor(n)
                 maps[(n, step[2])] = product(n, step[2], repeated[n])
                 carry(n, step[2])
             elif n == IMAGES - 1 and step[2] == (6, 7):
@@ -353,7 +356,6 @@ def tile_fast2order_de_conv_kernel(tc, x, W, out):
                     advance_w(s)
                     if s == 1:
                         repeated[1] = repeat_first_factor(1)
-                        aligned_second[1] = align_second_factor(1)
             s = index - FIRST_W_STEP
             if 0 <= s <= LAST:
                 quantise_w(s)
@@ -365,7 +367,7 @@ def tile_fast2order_de_conv_kernel(tc, x, W, out):
                     multiply_pass(1, len(early), (0,))
                     early.append(len(early))
                 advance_w(s + W_AHEAD)
-                if s == 0:
+                if s == 3:
                     repeated[2] = repeat_first_factor(2)
                     aligned_second[2] = align_second_factor(2)
                 if s == LAST:

@@ -54,7 +54,7 @@ LAST = len(PASSES) - 1
 IMAGE_GROUPS = ((0, 1), (1, 2), (2, IMAGES))
 COLUMN_GROUPS = (((0, 512), (512, 512)),) * (IMAGES - 1) + (((0, 512), (512, 256), (768, 256)),)
 RING = 12
-FIRST_W_STEP = 3
+FIRST_W_STEP = 5
 LAST_W_STEP = FIRST_W_STEP + LAST
 W_AHEAD = 4
 
@@ -90,13 +90,7 @@ def tile_fast2order_de_conv_kernel(tc, x, W, out):
 
         def load_w():
             for h in range(2):
-                for half in range(2):
-                    nc.gpsimd.dma_start(
-                        out=w_rows[:, h, half * 2048 : (half + 1) * 2048],
-                        in_=w_view[:, h, half * 2048 : (half + 1) * 2048],
-                    )
-
-        load_w()
+                nc.sync.dma_start(out=w_rows[:, h, :], in_=w_view[:, h, :])
 
         ident_bf16 = resident.tile([P, P], BF16, name="ident_bf16")
         make_identity(nc, ident_bf16[:])
@@ -138,12 +132,10 @@ def tile_fast2order_de_conv_kernel(tc, x, W, out):
             flat = tiles[g][:, n - IMAGE_GROUPS[g][0], :]
             return flat[:, row * SIDE : (row + rows) * SIDE].rearrange("p (r z) -> p r z", z=SIDE)
 
-        def load_x(g):
-            load_first(g)
-            load_second(g)
-
-        load_x(0)
-        load_x(1)
+        load_first(0)
+        load_second(0)
+        load_w()
+        load_first(1)
 
         w_codes = resident.tile([P, 2048], U32, name="w_codes", align_bytes=64)
         w_scales = resident.tile([P, 2048], U8, name="w_scales", align_bytes=64)
@@ -351,7 +343,9 @@ def tile_fast2order_de_conv_kernel(tc, x, W, out):
                     for s in step[2]:
                         multiply_all(n, s)
             if index == 1:
-                load_x(2)
+                load_second(1)
+                load_first(2)
+                load_second(2)
                 for s in range(W_AHEAD):
                     advance_w(s)
                     if s == 1:
@@ -367,7 +361,7 @@ def tile_fast2order_de_conv_kernel(tc, x, W, out):
                     multiply_pass(1, len(early), (0,))
                     early.append(len(early))
                 advance_w(s + W_AHEAD)
-                if s == 3:
+                if s == 0:
                     repeated[2] = repeat_first_factor(2)
                     aligned_second[2] = align_second_factor(2)
                 if s == LAST:

@@ -17,7 +17,6 @@ SIDE = 35
 GRID = 32
 ROW = 4 * GRID
 X_PITCH = 1232
-ALIGNED_PITCH = 40
 
 A, B, Y, Z = range(4)
 MAP_ROWS = 35
@@ -78,7 +77,6 @@ def tile_fast2order_de_conv_kernel(tc, x, W, out):
         repeated_pool = ctx.enter_context(tc.tile_pool(name="repeated", bufs=2))
         product_pool = ctx.enter_context(tc.tile_pool(name="products", bufs=1))
         carried_pool = ctx.enter_context(tc.tile_pool(name="carried", bufs=2))
-        aligned_pool = ctx.enter_context(tc.tile_pool(name="aligned", bufs=2))
         ring = ctx.enter_context(tc.tile_pool(name="ring", bufs=RING))
         w_stage = ctx.enter_context(tc.tile_pool(name="w_stage", bufs=3))
         result_pool = ctx.enter_context(tc.tile_pool(name="results", bufs=4))
@@ -150,31 +148,16 @@ def tile_fast2order_de_conv_kernel(tc, x, W, out):
                 nc.scalar.copy(out=pairs[:], in_=columns.to_broadcast([P, 4, MAP_ROWS, 8, 2]))
             return pairs
 
-        def align_second_factor(n):
-            rows = image_rows(second, n, 0, MAP_ROWS)
-            tiles = []
-            for odd in range(2):
-                aligned = aligned_pool.tile([P, MAP_ROWS, ALIGNED_PITCH], BF16, name="aligned%d" % odd)
-                copy = nc.vector.tensor_copy if n < 2 else nc.scalar.copy
-                copy(out=aligned[:, :, 0:34], in_=rows[:, :, odd : odd + 34])
-                tiles.append(aligned)
-            return tiles
-
         def product(n, k, pairs):
             rows = PRODUCT_ROWS[k]
             m = product_pool.tile([P, MAP_ROWS * ROW], BF16, name="map%d" % k, align_bytes=64)
             by_q = m[:].rearrange("p (r q e) -> p r q e", q=4, e=GRID)
-            if n in aligned_second:
-                low = FIRST_DISTANCE[k]
-                factors = [aligned_second[n][q % 2][:, low : low + rows, q - q % 2 : q - q % 2 + GRID] for q in range(4)]
-            else:
-                factor = image_rows(second, n, FIRST_DISTANCE[k], rows)
-                factors = [factor[:, :, q : q + GRID] for q in range(4)]
+            factor = image_rows(second, n, FIRST_DISTANCE[k], rows)
             for q in range(4):
                 nc.vector.tensor_tensor(
                     out=by_q[:, 0:rows, q, :].rearrange("p r (w t u) -> p r w t u", t=2, u=2),
                     in0=pairs[:, q, 0:rows].unsqueeze(3).to_broadcast([P, rows, 8, 2, 2]),
-                    in1=factors[q].rearrange("p r (w t u) -> p r w t u", t=2, u=2),
+                    in1=factor[:, :, q : q + GRID].rearrange("p r (w t u) -> p r w t u", t=2, u=2),
                     op=mybir.AluOpType.mult,
                 )
             return m
@@ -306,7 +289,6 @@ def tile_fast2order_de_conv_kernel(tc, x, W, out):
                 queue.dma_start(out=rows.rearrange("o y z -> o (y z)"), in_=res[:])
 
         repeated = {0: repeat_first_factor(0)}
-        aligned_second = {}
         maps = {}
         sums_of = {}
         quantised = {}
@@ -326,8 +308,6 @@ def tile_fast2order_de_conv_kernel(tc, x, W, out):
         for index, step in enumerate(vector_steps()):
             n = step[1]
             if step[0] == "product":
-                if step[2] == A and n < 2:
-                    aligned_second[n] = align_second_factor(n)
                 maps[(n, step[2])] = product(n, step[2], repeated[n])
                 carry(n, step[2])
             elif n == IMAGES - 1 and step[2] == (6, 7):
@@ -355,7 +335,6 @@ def tile_fast2order_de_conv_kernel(tc, x, W, out):
                 quantise_w(s)
                 if s == LAST:
                     repeated[3] = repeat_first_factor(3)
-                    aligned_second[3] = align_second_factor(3)
                 multiply_all(0, s)
                 while len(early) < LAST and len(early) <= s and (1, len(early)) in quantised:
                     multiply_pass(1, len(early), (0,))
@@ -363,7 +342,6 @@ def tile_fast2order_de_conv_kernel(tc, x, W, out):
                 advance_w(s + W_AHEAD)
                 if s == 0:
                     repeated[2] = repeat_first_factor(2)
-                    aligned_second[2] = align_second_factor(2)
                 if s == LAST:
                     for s1 in range(LAST + 1):
                         if (1, s1) in quantised:

@@ -122,8 +122,16 @@ def tile_fast2order_de_conv_kernel(tc, x, W, out):
         def load_first(g):
             load_shifted(first, g, lambda v: SIDE * SIDE - 3, lambda a, v: a)
 
-        def load_second(g):
-            load_shifted(second, g, lambda v: (SIDE - v) * SIDE, lambda a, v: v * SIDE)
+        def load_second(g, queue=nc.sync):
+            n0, n1 = IMAGE_GROUPS[g]
+            for n in range(n0, n1):
+                for v in range(2):
+                    length = (SIDE - v) * SIDE
+                    rows = x_cn[:, n, v * SIDE : v * SIDE + length]
+                    queue.dma_start(
+                        out=second[g][v:P:2, n - n0, 0:length],
+                        in_=rows.unsqueeze(1).to_broadcast([16, 4, length]),
+                    )
 
         def image_rows(tiles, n, row, rows):
             g = min(n, len(IMAGE_GROUPS) - 1)

@@ -42,10 +42,10 @@ PASSES = (
 
 def window_rows(m, r):
     return {
-        A: ((r, r), (r, r + 1)),
-        B: ((r, r + 2), (r, r + 3)),
-        Z: ((r, r + 1), (r + 2, r + 2)),
-        Y: ((r + 1, r + 3), (r + 2, r + 3)),
+        A: ((r, r), (r + 1, r)),
+        B: ((r + 2, r), (r + 3, r)),
+        Z: ((r + 1, r), (r + 2, r + 2)),
+        Y: ((r + 3, r + 1), (r + 3, r + 2)),
     }[m]
 
 
@@ -103,35 +103,35 @@ def tile_fast2order_de_conv_kernel(tc, x, W, out):
             resident.tile([P, n1 - n0, X_PITCH], BF16, name="second_%d" % n0) for (n0, n1) in IMAGE_GROUPS
         ]
         unused = (SIDE - 1) * SIDE // 16 * 16
-        for tile in second:
-            nc.vector.memset(tile[:, :, unused:X_PITCH], 0.0)
+        nc.vector.memset(first[-1][:, :, unused:X_PITCH], 0.0)
 
         warm = resident.tile([P, 2], BF16, name="warm")
-        nc.scalar.copy(out=warm[:], in_=second[0][:, 0, X_PITCH - 2 : X_PITCH])
+        nc.scalar.copy(out=warm[:], in_=first[-1][:, 0, X_PITCH - 2 : X_PITCH])
 
-        def load_shifted(tiles, g, length, shift):
-            n0, n1 = IMAGE_GROUPS[g]
-            for a in range(4):
-                for v in range(2):
-                    start = shift(a, v)
-                    nc.sync.dma_start(
-                        out=tiles[g][2 * a + v : P : 8, :, 0 : length(v)],
-                        in_=x_cn[:, n0:n1, start : start + length(v)],
-                    )
+        x_flat = x.rearrange("n c h w -> (n c h w)")
+        image_size = 16 * SIDE * SIDE
 
         def load_first(g):
-            load_shifted(first, g, lambda v: SIDE * SIDE - 3, lambda a, v: a)
+            n0, n1 = IMAGE_GROUPS[g]
+            for v in range(2):
+                for a in range(4):
+                    start = v * SIDE + a
+                    if n1 < IMAGES:
+                        length = SIDE * SIDE - 3
+                        at = n0 * image_size + start
+                        rows = x_flat[at : at + image_size].rearrange("(c l) -> c l", c=16)[:, 0:length].unsqueeze(1)
+                    else:
+                        length = (SIDE - v) * SIDE - 3
+                        rows = x_cn[:, n0:n1, start : start + length]
+                    nc.sync.dma_start(out=first[g][2 * a + v : P : 8, :, 0:length], in_=rows)
 
         def load_second(g, queue=nc.sync):
             n0, n1 = IMAGE_GROUPS[g]
             for n in range(n0, n1):
-                for v in range(2):
-                    length = (SIDE - v) * SIDE
-                    rows = x_cn[:, n, v * SIDE : v * SIDE + length]
-                    queue.dma_start(
-                        out=second[g][v:P:2, n - n0, 0:length],
-                        in_=rows.unsqueeze(1).to_broadcast([16, 4, length]),
-                    )
+                queue.dma_start(
+                    out=second[g][:, n - n0, 0 : SIDE * SIDE],
+                    in_=x_cn[:, n, :].unsqueeze(1).to_broadcast([16, 8, SIDE * SIDE]),
+                )
 
         def image_rows(tiles, n, row, rows):
             g = min(n, len(IMAGE_GROUPS) - 1)
@@ -160,11 +160,12 @@ def tile_fast2order_de_conv_kernel(tc, x, W, out):
             rows = PRODUCT_ROWS[k]
             m = product_pool.tile([P, MAP_ROWS * ROW], BF16, name="map%d" % k, align_bytes=64)
             by_q = m[:].rearrange("p (r q e) -> p r q e", q=4, e=GRID)
-            factor = image_rows(second, n, FIRST_DISTANCE[k], rows)
+            factor = image_rows(second, n, 0, rows)
+            distance = FIRST_DISTANCE[k]
             for q in range(4):
                 nc.vector.tensor_tensor(
                     out=by_q[:, 0:rows, q, :].rearrange("p r (w t u) -> p r w t u", t=2, u=2),
-                    in0=pairs[:, q, 0:rows].unsqueeze(3).to_broadcast([P, rows, 8, 2, 2]),
+                    in0=pairs[:, q, distance : distance + rows].unsqueeze(3).to_broadcast([P, rows, 8, 2, 2]),
                     in1=factor[:, :, q : q + GRID].rearrange("p r (w t u) -> p r w t u", t=2, u=2),
                     op=mybir.AluOpType.mult,
                 )

@@ -50,6 +50,7 @@ def window_rows(m, r):
 
 
 LAST = len(PASSES) - 1
+EARLY_ROWS = ((0, 9), (9, SIDE))
 IMAGE_GROUPS = ((0, 1), (1, 2), (2, IMAGES))
 COLUMN_GROUPS = (((0, 512), (512, 512)),) * (IMAGES - 1) + (((0, 512), (512, 256), (768, 256)),)
 RING = 12
@@ -64,7 +65,7 @@ def vector_steps():
         steps += [("quantise", n, (0, 1)), ("quantise", n, (2, 3))]
         if 0 < n < IMAGES - 1:
             steps += [("product", n + 1, A), ("product", n + 1, B)]
-        steps += [("quantise", n, (4, 5)), ("quantise", n, (6, 7))]
+        steps += [("quantise", n, (4, 5)), ("quantise", n, (6, 7))] if n < IMAGES - 1 else [("quantise", n, (4, 5, 6, 7))]
         if n == 0:
             steps += [("product", 1, A), ("product", 1, B)]
     return steps
@@ -100,7 +101,7 @@ def tile_fast2order_de_conv_kernel(tc, x, W, out):
             resident.tile([P, n1 - n0, X_PITCH], BF16, name="first_%d" % n0) for (n0, n1) in IMAGE_GROUPS
         ]
         second = [
-            resident.tile([P, n1 - n0, X_PITCH], BF16, name="second_%d" % n0) for (n0, n1) in IMAGE_GROUPS
+            resident.tile([P, n1 - n0, X_PITCH], BF16, name="second_%d" % n0) for (n0, n1) in IMAGE_GROUPS[1:]
         ]
         unused = (SIDE - 1) * SIDE // 16 * 16
         nc.vector.memset(first[-1][:, :, unused:X_PITCH], 0.0)
@@ -125,17 +126,32 @@ def tile_fast2order_de_conv_kernel(tc, x, W, out):
                         rows = x_cn[:, n0:n1, start : start + length]
                     nc.sync.dma_start(out=first[g][2 * a + v : P : 8, :, 0:length], in_=rows)
 
-        def load_second(g, queue=nc.sync):
+        early_rows = [
+            resident.tile([P, 1, X_PITCH], BF16, name="early_%d" % row) for (row, end) in EARLY_ROWS
+        ]
+
+        def load_rows(tile, n, row, end):
+            values = (end - row) * SIDE
+            nc.sync.dma_start(
+                out=tile[:, 0:values],
+                in_=x_cn[:, n, row * SIDE : row * SIDE + values].unsqueeze(1).to_broadcast([16, 8, values]),
+            )
+
+        def load_second(g):
             n0, n1 = IMAGE_GROUPS[g]
-            for n in range(n0, n1):
-                queue.dma_start(
-                    out=second[g][:, n - n0, 0 : SIDE * SIDE],
-                    in_=x_cn[:, n, :].unsqueeze(1).to_broadcast([16, 8, SIDE * SIDE]),
-                )
+            if g == 0:
+                for tile, (row, end) in zip(early_rows, EARLY_ROWS):
+                    load_rows(tile[:, 0, :], 0, row, end)
+            else:
+                for n in range(n0, n1):
+                    load_rows(second[g - 1][:, n - n0, :], n, 0, SIDE)
 
         def image_rows(tiles, n, row, rows):
             g = min(n, len(IMAGE_GROUPS) - 1)
             flat = tiles[g][:, n - IMAGE_GROUPS[g][0], :]
+            return row_view(flat, row, rows)
+
+        def row_view(flat, row, rows):
             return flat[:, row * SIDE : (row + rows) * SIDE].rearrange("p (r z) -> p r z", z=SIDE)
 
         load_first(0)
@@ -160,12 +176,19 @@ def tile_fast2order_de_conv_kernel(tc, x, W, out):
             rows = PRODUCT_ROWS[k]
             m = product_pool.tile([P, MAP_ROWS * ROW], BF16, name="map%d" % k, align_bytes=64)
             by_q = m[:].rearrange("p (r q e) -> p r q e", q=4, e=GRID)
-            factor = image_rows(second, n, 0, rows)
-            distance = FIRST_DISTANCE[k]
-            for q in range(4):
+            if n == 0:
+                factors = [
+                    (row, min(end, rows), row_view(tile[:, 0, :], 0, min(end, rows) - row))
+                    for tile, (row, end) in zip(early_rows, EARLY_ROWS)
+                ]
+            else:
+                factors = [(0, rows, row_view(second[min(n, 2) - 1][:, max(n - 2, 0), :], 0, rows))]
+            for (row, end, factor), q in [(f, q) for f in factors for q in range(4)]:
+                first_row = FIRST_DISTANCE[k] + row
+                count = end - row
                 nc.vector.tensor_tensor(
-                    out=by_q[:, 0:rows, q, :].rearrange("p r (w t u) -> p r w t u", t=2, u=2),
-                    in0=pairs[:, q, distance : distance + rows].unsqueeze(3).to_broadcast([P, rows, 8, 2, 2]),
+                    out=by_q[:, row:end, q, :].rearrange("p r (w t u) -> p r w t u", t=2, u=2),
+                    in0=pairs[:, q, first_row : first_row + count].unsqueeze(3).to_broadcast([P, count, 8, 2, 2]),
                     in1=factor[:, :, q : q + GRID].rearrange("p r (w t u) -> p r w t u", t=2, u=2),
                     op=mybir.AluOpType.mult,
                 )
@@ -319,7 +342,7 @@ def tile_fast2order_de_conv_kernel(tc, x, W, out):
             if step[0] == "product":
                 maps[(n, step[2])] = product(n, step[2], repeated[n])
                 carry(n, step[2])
-            elif n == IMAGES - 1 and step[2] == (6, 7):
+            elif n == IMAGES - 1 and LAST in step[2]:
                 for g, (start, columns) in enumerate(COLUMN_GROUPS[n]):
                     for s in step[2]:
                         codes, scales = quantise(maps[(n, PASSES[s][0])], PASSES[s][1], start, columns)

@@ -80,7 +80,7 @@ def tile_fast2order_de_conv_kernel(tc, x, W, out):
         carried_pool = ctx.enter_context(tc.tile_pool(name="carried", bufs=2))
         ring = ctx.enter_context(tc.tile_pool(name="ring", bufs=RING))
         w_stage = ctx.enter_context(tc.tile_pool(name="w_stage", bufs=3))
-        result_pool = ctx.enter_context(tc.tile_pool(name="results", bufs=4))
+        result_pool = ctx.enter_context(tc.tile_pool(name="results", bufs=2))
         banks = ctx.enter_context(tc.psum_pool(name="banks", bufs=8))
         ctx.enter_context(tc.manual_schedule())
 
@@ -207,7 +207,7 @@ def tile_fast2order_de_conv_kernel(tc, x, W, out):
 
         def quantise(m, r, start=0, columns=1024):
             at = r * ROW + 4 * start
-            depth = RING if columns == 1024 else 4
+            depth = {1024: RING, 512: 4, 256: 8}[columns]
             codes = ring.tile([P, columns], U32, name="codes%d" % columns, align_bytes=64, bufs=depth)
             scales = ring.tile([P, columns], U8, name="scales%d" % columns, align_bytes=64, bufs=depth)
             nc.vector.quantize_mx(
@@ -308,17 +308,17 @@ def tile_fast2order_de_conv_kernel(tc, x, W, out):
 
         def store(n, g):
             start, columns = COLUMN_GROUPS[n][g]
+            res = result_pool.tile([P, 2, columns], F32, name="res%d" % columns)
             for h in range(2):
-                res = result_pool.tile([P, columns], F32, name="res%d" % columns)
-                dst = res[:].rearrange("p (y w q) -> p y w q", w=8, q=4)
+                dst = res[:, h, :].rearrange("p (y w q) -> p y w q", w=8, q=4)
                 src = sums_of[(n, g, h)][:, 0:columns].rearrange("p (y q w) -> p y w q", q=4, w=8)
-                rows = out[n, h * P : (h + 1) * P, start // GRID : (start + columns) // GRID, :]
                 if n == IMAGES - 1 and g == len(COLUMN_GROUPS[n]) - 1 and h == 1:
                     nc.vector.tensor_copy(out=dst, in_=src)
                 else:
                     nc.scalar.copy(out=dst, in_=src)
-                queue = nc.sync if n == IMAGES - 1 else nc.scalar
-                queue.dma_start(out=rows.rearrange("o y z -> o (y z)"), in_=res[:])
+            queue = nc.sync if n == IMAGES - 1 else nc.scalar
+            rows = out[n, :, start // GRID : (start + columns) // GRID, :]
+            queue.dma_start(out=rows.rearrange("(h o) y z -> o h (y z)", h=2), in_=res[:])
 
         repeated = {0: repeat_first_factor(0)}
         maps = {}

from contextlib import ExitStack

import concourse.mybir as mybir
from concourse.masks import make_identity

FLOPS = 2 * 256 * 4096 * 4096

BF16 = mybir.dt.bfloat16
F32 = mybir.dt.float32
U32 = mybir.dt.uint32
U8 = mybir.dt.uint8
FP8X4 = mybir.dt.float8_e4m3fn_x4

P = 128
IMAGES = 4
SIDE = 35
GRID = 32
ROW = 4 * GRID
X_PITCH = 1232

A, B, Y, Z = range(4)
MAP_ROWS = 35
PRODUCT_ROWS = (35, 33)
FIRST_DISTANCE = (0, 2)
CARRIED = (
    (Z, 0, A, 1, 0, 33),
    (Z, 1, A, 0, 2, 33),
    (Y, 1, A, 1, 2, 32),
    (Y, 0, B, 0, 1, 32),
)
PASSES = (
    (A, 0, False),
    (A, 1, False),
    (B, 0, False),
    (B, 0, True),
    (Z, 0, True),
    (Z, 1, True),
    (Y, 0, False),
    (Y, 0, True),
)


def window_rows(m, r):
    return {
        A: ((r, r), (r + 1, r)),
        B: ((r + 2, r), (r + 3, r)),
        Z: ((r + 1, r), (r + 2, r + 2)),
        Y: ((r + 3, r + 1), (r + 3, r + 2)),
    }[m]


LAST = len(PASSES) - 1
EARLY_ROWS = ((0, 9), (9, SIDE))
IMAGE_GROUPS = ((0, 1), (1, 2), (2, IMAGES))
COLUMN_GROUPS = (((0, 512), (512, 512)),) * (IMAGES - 1) + (((0, 512), (512, 256), (768, 256)),)
RING = 12
FIRST_W_STEP = 5
LAST_W_STEP = FIRST_W_STEP + LAST
W_AHEAD = 4


def vector_steps():
    steps = [("product", 0, A), ("product", 0, B)]
    for n in range(IMAGES):
        steps += [("quantise", n, (0, 1)), ("quantise", n, (2, 3))]
        if 0 < n < IMAGES - 1:
            steps += [("product", n + 1, A), ("product", n + 1, B)]
        steps += [("quantise", n, (4, 5)), ("quantise", n, (6, 7))] if n < IMAGES - 1 else [("quantise", n, (4, 5, 6, 7))]
        if n == 0:
            steps += [("product", 1, A), ("product", 1, B)]
    return steps


def tile_fast2order_de_conv_kernel(tc, x, W, out):
    nc = tc.nc
    with ExitStack() as ctx:
        resident = ctx.enter_context(tc.tile_pool(name="resident", bufs=1))
        repeated_pool = ctx.enter_context(tc.tile_pool(name="repeated", bufs=2))
        product_pool = ctx.enter_context(tc.tile_pool(name="products", bufs=1))
        carried_pool = ctx.enter_context(tc.tile_pool(name="carried", bufs=2))
        ring = ctx.enter_context(tc.tile_pool(name="ring", bufs=RING))
        w_stage = ctx.enter_context(tc.tile_pool(name="w_stage", bufs=3))
        result_pool = ctx.enter_context(tc.tile_pool(name="results", bufs=2))
        banks = ctx.enter_context(tc.psum_pool(name="banks", bufs=8))
        ctx.enter_context(tc.manual_schedule())

        w_rows = resident.tile([P, 2, 4096], BF16, name="w_rows")
        w_view = W.rearrange("(h o) f -> o h f", h=2)

        def load_w():
            for h in range(2):
                nc.sync.dma_start(out=w_rows[:, h, :], in_=w_view[:, h, :])

        ident_bf16 = resident.tile([P, P], BF16, name="ident_bf16")
        make_identity(nc, ident_bf16[:])
        ident_f32 = resident.tile([P, P], F32, name="ident_f32")
        make_identity(nc, ident_f32[:])

        x_cn = x.rearrange("n c h w -> c n (h w)")
        first = [
            resident.tile([P, n1 - n0, X_PITCH], BF16, name="first_%d" % n0) for (n0, n1) in IMAGE_GROUPS
        ]
        second = [
            resident.tile([P, n1 - n0, X_PITCH], BF16, name="second_%d" % n0) for (n0, n1) in IMAGE_GROUPS[1:]
        ]
        unused = (SIDE - 1) * SIDE // 16 * 16
        nc.vector.memset(first[-1][:, :, unused:X_PITCH], 0.0)

        warm = resident.tile([P, 2], BF16, name="warm")
        nc.scalar.copy(out=warm[:], in_=first[-1][:, 0, X_PITCH - 2 : X_PITCH])

        x_flat = x.rearrange("n c h w -> (n c h w)")
        image_size = 16 * SIDE * SIDE

        def load_first(g):
            n0, n1 = IMAGE_GROUPS[g]
            for v in range(2):
                for a in range(4):
                    start = v * SIDE + a
                    if n1 < IMAGES:
                        length = SIDE * SIDE - 3
                        at = n0 * image_size + start
                        rows = x_flat[at : at + image_size].rearrange("(c l) -> c l", c=16)[:, 0:length].unsqueeze(1)
                    else:
                        length = (SIDE - v) * SIDE - 3
                        rows = x_cn[:, n0:n1, start : start + length]
                    nc.sync.dma_start(out=first[g][2 * a + v : P : 8, :, 0:length], in_=rows)

        early_rows = [
            resident.tile([P, 1, X_PITCH], BF16, name="early_%d" % row) for (row, end) in EARLY_ROWS
        ]

        def load_rows(tile, n, row, end):
            values = (end - row) * SIDE
            nc.sync.dma_start(
                out=tile[:, 0:values],
                in_=x_cn[:, n, row * SIDE : row * SIDE + values].unsqueeze(1).to_broadcast([16, 8, values]),
            )

        def load_second(g):
            n0, n1 = IMAGE_GROUPS[g]
            if g == 0:
                for tile, (row, end) in zip(early_rows, EARLY_ROWS):
                    load_rows(tile[:, 0, :], 0, row, end)
            else:
                for n in range(n0, n1):
                    load_rows(second[g - 1][:, n - n0, :], n, 0, SIDE)

        def image_rows(tiles, n, row, rows):
            g = min(n, len(IMAGE_GROUPS) - 1)
            flat = tiles[g][:, n - IMAGE_GROUPS[g][0], :]
            return row_view(flat, row, rows)

        def row_view(flat, row, rows):
            return flat[:, row * SIDE : (row + rows) * SIDE].rearrange("p (r z) -> p r z", z=SIDE)

        load_first(0)
        load_second(0)
        load_w()
        load_first(1)

        w_codes = resident.tile([P, 2048], U32, name="w_codes", align_bytes=64)
        w_scales = resident.tile([P, 2048], U8, name="w_scales", align_bytes=64)

        def repeat_first_factor(n):
            pairs = repeated_pool.tile([P, 4, MAP_ROWS, 8, 2], BF16, name="pairs")
            columns = image_rows(first, n, 0, MAP_ROWS)[:, :, 0:GRID].rearrange("p r (w q) -> p q r w", q=4).unsqueeze(4)
            if n == 0:
                nc.vector.tensor_copy(out=pairs[:, 0:2], in_=columns[:, 0:2].to_broadcast([P, 2, MAP_ROWS, 8, 2]))
                nc.scalar.copy(out=pairs[:, 2:4], in_=columns[:, 2:4].to_broadcast([P, 2, MAP_ROWS, 8, 2]))
            else:
                nc.scalar.copy(out=pairs[:], in_=columns.to_broadcast([P, 4, MAP_ROWS, 8, 2]))
            return pairs

        def product(n, k, pairs):
            rows = PRODUCT_ROWS[k]
            m = product_pool.tile([P, MAP_ROWS * ROW], BF16, name="map%d" % k, align_bytes=64)
            by_q = m[:].rearrange("p (r q e) -> p r q e", q=4, e=GRID)
            if n == 0:
                factors = [
                    (row, min(end, rows), row_view(tile[:, 0, :], 0, min(end, rows) - row))
                    for tile, (row, end) in zip(early_rows, EARLY_ROWS)
                ]
            else:
                factors = [(0, rows, row_view(second[min(n, 2) - 1][:, max(n - 2, 0), :], 0, rows))]
            for (row, end, factor), q in [(f, q) for f in factors for q in range(4)]:
                first_row = FIRST_DISTANCE[k] + row
                count = end - row
                nc.vector.tensor_tensor(
                    out=by_q[:, row:end, q, :].rearrange("p r (w t u) -> p r w t u", t=2, u=2),
                    in0=pairs[:, q, first_row : first_row + count].unsqueeze(3).to_broadcast([P, count, 8, 2, 2]),
                    in1=factor[:, :, q : q + GRID].rearrange("p r (w t u) -> p r w t u", t=2, u=2),
                    op=mybir.AluOpType.mult,
                )
            return m

        def carry(n, k):
            for to, to_v, source, from_v, row, rows in CARRIED:
                if source != k:
                    continue
                if (n, to) not in maps:
                    maps[(n, to)] = carried_pool.tile([P, 33 * ROW], BF16, name="map%d" % to, align_bytes=64)
                nc.sync.dma_start(
                    out=maps[(n, to)][to_v:P:2, 0 : rows * ROW],
                    in_=maps[(n, source)][from_v:P:2, row * ROW : (row + rows) * ROW],
                )

        def quantise(m, r, start=0, columns=1024):
            at = r * ROW + 4 * start
            depth = {1024: RING, 512: 4, 256: 8}[columns]
            codes = ring.tile([P, columns], U32, name="codes%d" % columns, align_bytes=64, bufs=depth)
            scales = ring.tile([P, columns], U8, name="scales%d" % columns, align_bytes=64, bufs=depth)
            nc.vector.quantize_mx(
                out=codes[:].bitcast(FP8X4),
                scales=scales[:],
                in_=m[:, at : at + 4 * columns],
            )
            return codes, scales

        w_bf16 = w_rows[:].rearrange("p h (c i a j t) -> p (h c) i a j t", c=16, i=4, a=4, j=4, t=4)
        w_pairs = w_rows[:].bitcast(F32).rearrange("p h (c i a j u) -> p (h c) i a j u", c=16, i=4, a=4, j=4, u=2)
        sorted_w = {}
        transposed_w = {}
        grouped_w = {}

        def sort_w(s):
            m, r, exchanged = PASSES[s]
            if exchanged:
                cols = w_stage.tile([P, 4, 2, P], BF16, name="w_cols")
            else:
                cols = w_stage.tile([P, 2, 2, P], F32, name="w_col_pairs")
            by_v = cols[:].rearrange("p t h (c a v) -> p t (h c) a v", a=4, v=2)
            (a0, t0), (a1, t1) = window_rows(m, r)
            if a0 != a1 and t0 != t1:
                for v, (row_a, row_t) in enumerate(window_rows(m, r)):
                    dst = by_v[:, :, :, :, v]
                    if exchanged:
                        src = w_bf16[:, :, row_t, :, row_a, :].rearrange("p g t a -> p t g a")
                    else:
                        src = w_pairs[:, :, row_a, :, row_t, :]
                        dst = dst.rearrange("p u g a -> p g a u")
                    nc.scalar.copy(out=dst, in_=src)
            else:
                row_a = a0 if a0 == a1 else slice(a0, a1 + 1)
                row_t = t0 if t0 == t1 else slice(t0, t1 + 1)
                if exchanged:
                    src = w_bf16[:, :, row_t, :, row_a, :]
                    src = src.rearrange("p g t v a -> p t g a v" if t0 == t1 else "p g v t a -> p t g a v")
                    nc.scalar.copy(out=by_v, in_=src)
                else:
                    src = w_pairs[:, :, row_a, :, row_t, :]
                    if a0 != a1:
                        src = src.rearrange("p g v a u -> p g a v u")
                    nc.scalar.copy(out=by_v.rearrange("p u g a v -> p g a v u"), in_=src)
            sorted_w[s] = cols

        def transpose_w(s):
            exchanged = PASSES[s][2]
            if exchanged:
                bank = banks.tile([P, 4, 2, P], BF16, name="w_t", tag="bank")
            else:
                bank = banks.tile([P, 2, 2, P], F32, name="w_t_pairs", tag="bank")
            for t in range(4 if exchanged else 2):
                for h in range(2):
                    nc.tensor.transpose(
                        bank[:, t, h, :], sorted_w[s][:, t, h, :], ident_bf16[:] if exchanged else ident_f32[:]
                    )
            transposed_w[s] = bank

        def group_w(s):
            grouped = w_stage.tile([P, 1024], BF16, name="w_grouped", align_bytes=64, bufs=4)
            if PASSES[s][2]:
                dst = grouped[:].rearrange("p (h o t) -> p h o t", h=2, t=4)
            else:
                dst = grouped[:].bitcast(F32).rearrange("p (h o t) -> p h o t", h=2, t=2)
            nc.scalar.copy(out=dst, in_=transposed_w[s][:].rearrange("p t h o -> p h o t"))
            grouped_w[s] = grouped

        def advance_w(s):
            if s <= LAST:
                sort_w(s)
                transpose_w(s)
            if 1 <= s <= LAST + 1:
                group_w(s - 1)

        def quantise_w(s):
            nc.vector.quantize_mx(
                out=w_codes[:, s * 256 : (s + 1) * 256].bitcast(FP8X4),
                scales=w_scales[:, s * 256 : (s + 1) * 256],
                in_=grouped_w[s][:],
            )

        def multiply(n, s, g, codes, scales, at):
            columns = COLUMN_GROUPS[n][g][1]
            for h in range(2):
                if s == 0:
                    sums_of[(n, g, h)] = banks.tile([P, 512], F32, name="sums", tag="bank")
                lo = s * 256 + h * P
                nc.tensor.matmul_mx(
                    out=sums_of[(n, g, h)][:, 0:columns],
                    lhsT=w_codes[:, lo : lo + P].bitcast(FP8X4),
                    lhsT_scale=w_scales[:, lo : lo + P],
                    rhs=codes[:, at : at + columns].bitcast(FP8X4),
                    rhs_scale=scales[:, at : at + columns],
                    start=(s == 0),
                    stop=(s == LAST),
                )

        def store(n, g):
            start, columns = COLUMN_GROUPS[n][g]
            res = result_pool.tile([P, 2, columns], F32, name="res%d" % columns)
            for h in range(2):
                dst = res[:, h, :].rearrange("p (y w q) -> p y w q", w=8, q=4)
                src = sums_of[(n, g, h)][:, 0:columns].rearrange("p (y q w) -> p y w q", q=4, w=8)
                if n == IMAGES - 1 and g == len(COLUMN_GROUPS[n]) - 1 and h == 1:
                    nc.vector.tensor_copy(out=dst, in_=src)
                else:
                    nc.scalar.copy(out=dst, in_=src)
            queue = nc.sync if n == IMAGES - 1 else nc.scalar
            rows = out[n, :, start // GRID : (start + columns) // GRID, :]
            queue.dma_start(out=rows.rearrange("(h o) y z -> o h (y z)", h=2), in_=res[:])

        repeated = {0: repeat_first_factor(0)}
        maps = {}
        sums_of = {}
        quantised = {}

        def multiply_pass(n, s, groups):
            codes, scales = quantised[(n, s)]
            for g in groups:
                multiply(n, s, g, codes, scales, COLUMN_GROUPS[n][g][0])
                if s == LAST:
                    store(n, g)

        def multiply_all(n, s):
            multiply_pass(n, s, range(len(COLUMN_GROUPS[n])))

        early = []

        for index, step in enumerate(vector_steps()):
            n = step[1]
            if step[0] == "product":
                maps[(n, step[2])] = product(n, step[2], repeated[n])
                carry(n, step[2])
            elif n == IMAGES - 1 and LAST in step[2]:
                for g, (start, columns) in enumerate(COLUMN_GROUPS[n]):
                    for s in step[2]:
                        codes, scales = quantise(maps[(n, PASSES[s][0])], PASSES[s][1], start, columns)
                        multiply(n, s, g, codes, scales, 0)
                    store(n, g)
            else:
                for s in step[2]:
                    quantised[(n, s)] = quantise(maps[(n, PASSES[s][0])], PASSES[s][1])
                if index > LAST_W_STEP:
                    for s in step[2]:
                        multiply_all(n, s)
            if index == 1:
                load_second(1)
                load_first(2)
                load_second(2)
                for s in range(W_AHEAD):
                    advance_w(s)
                    if s == 1:
                        repeated[1] = repeat_first_factor(1)
            s = index - FIRST_W_STEP
            if 0 <= s <= LAST:
                quantise_w(s)
                if s == LAST:
                    repeated[3] = repeat_first_factor(3)
                multiply_all(0, s)
                while len(early) < LAST and len(early) <= s and (1, len(early)) in quantised:
                    multiply_pass(1, len(early), (0,))
                    early.append(len(early))
                advance_w(s + W_AHEAD)
                if s == 0:
                    repeated[2] = repeat_first_factor(2)
                if s == LAST:
                    for s1 in range(LAST + 1):
                        if (1, s1) in quantised:
                            multiply_pass(1, s1, (1,) if s1 in early else (0, 1))
